import numpy as np
import ml_dtypes


def mxq(x, axis, fmt="e4m3"):
    dtype, down = {"e4m3": (ml_dtypes.float8_e4m3fn, 7), "e5m2": (ml_dtypes.float8_e5m2, 14)}[fmt]
    v = np.moveaxis(np.asarray(x, np.float32).astype(ml_dtypes.bfloat16).astype(np.float64), axis, -1)
    blocks = v.reshape(v.shape[:-1] + (-1, 32))
    amax = np.abs(blocks).max(-1, keepdims=True)
    byte = np.maximum(np.where(amax > 0, np.frexp(amax)[1] - 1 + 127, 0) - down, 1)
    scale = np.exp2(byte - 127.0)
    codes = (blocks / scale).astype(np.float32).astype(dtype).astype(np.float64)
    return np.moveaxis((codes * scale).reshape(v.shape), -1, axis)


WIDE = False


def mx_kscale(k):
    if not WIDE:
        return np.ones(k)
    levels = np.array([10, -10, 5, -5, 0])
    a = np.random.permutation(np.resize(levels, k // 512 * 4)).reshape(k // 512, 4)
    idx = np.arange(k)
    return np.exp2(a[idx // 512, idx % 128 // 32])


BF16 = ml_dtypes.bfloat16


def bf(x):
    return np.asarray(x, np.float32).astype(BF16)


def f64(x):
    return np.asarray(x).astype(np.float64)


B, D, H = 512, 2048, 1024


def setup_inputs():
    s, t = mx_kscale(D), mx_kscale(H)
    return {"x": bf(np.random.standard_normal((B, D)) * s),
            "xz_o": bf(np.random.standard_normal((B, H)) * 0.7),
            "h_prev": bf(np.random.standard_normal((B, H)) * t),
            "c": bf(np.random.standard_normal((B, H)) * 0.65),
            "w_i": bf(np.random.standard_normal((D, H)) * 0.7 / np.sqrt(D) / s[:, None]),
            "w_ho": bf(np.random.standard_normal((H, H)) * 0.7 / np.sqrt(H) / t[:, None]),
            "w_co": bf(np.random.standard_normal((H, H)) * 0.7 / np.sqrt(H)),
            "w_c": bf(np.random.standard_normal((H, H)) * 0.7 / np.sqrt(H)),
            "b_o": bf(np.random.standard_normal(H) * 0.3)}


def reference(x, xz_o, h_prev, c, w_i, w_ho, w_co, w_c, b_o):
    cc = f64(c)
    o = f64(xz_o) + (mxq(f64(h_prev), 1, "e4m3") @ mxq(f64(w_ho), 0, "e4m3")) + (mxq(cc, 1, "e4m3") @ mxq(f64(w_co), 0, "e4m3")) + f64(b_o)
    return np.tanh(o) * ((mxq(np.tanh(cc), 1, "e4m3") @ mxq(f64(w_c), 0, "e4m3")) + (mxq(f64(x), 1, "e4m3") @ mxq(f64(w_i), 0, "e4m3")))

@@ -1,0 +1,228 @@
+from contextlib import ExitStack
+
+import concourse.mybir as mybir
+from concourse.masks import make_identity
+
+F32 = mybir.dt.float32
+BF16 = mybir.dt.bfloat16
+U32 = mybir.dt.uint32
+U8 = mybir.dt.uint8
+FP8X4 = mybir.dt.float8_e4m3fn_x4
+ADD = mybir.AluOpType.add
+MULT = mybir.AluOpType.mult
+TANH = mybir.ActivationFunctionType.Tanh
+
+B, D, H = 512, 2048, 1024
+P = 128
+PACK = 4
+K_PASS = P * PACK
+B_TILES = B // P
+BANK = 512
+HALVES = H // BANK
+
+FIRST_H = 0
+FIRST_C = 2
+FIRST_TANH_C = 4
+FIRST_X = 6
+PASSES = 10
+GATE_PASSES = (0, 1, 2, 3)
+PROJECTION_PASSES = (4, 5, 6, 7, 8, 9)
+
+W_RAW_BUFS = 5
+
+FLOPS = 2 * B * H * (H + H + H + D)
+
+
+def tile_residuallstmcell_pb_kernel(tc, x, xz_o, h_prev, c, w_i, w_ho, w_co, w_c, b_o, out):
+    nc = tc.nc
+    with ExitStack() as ctx:
+        keep = ctx.enter_context(tc.tile_pool(name="keep", bufs=1))
+        act_stage = ctx.enter_context(tc.tile_pool(name="act_stage", bufs=5))
+        w_raw_pool = ctx.enter_context(tc.tile_pool(name="w_raw", bufs=W_RAW_BUFS))
+        w_stage = ctx.enter_context(tc.tile_pool(name="w_stage", bufs=3))
+        psum = ctx.enter_context(tc.psum_pool(name="psum", bufs=8))
+
+        b_row = keep.tile([P, H], BF16, name="b_row")
+        nc.vector.memset(b_row[:], 0.0)
+        nc.sync.dma_start(out=b_row[0:1, :], in_=b_o.rearrange("(o n) -> o n", o=1))
+
+        def load_rows(src, width, name):
+            raw = keep.tile([P, B_TILES * width], BF16, name=name)
+            return raw, raw[:].rearrange("p (t k) -> p t k", t=B_TILES), src.rearrange("(p t) k -> p t k", t=B_TILES)
+
+        h_raw, h_dst, h_src = load_rows(h_prev, H, "h_raw")
+        c_raw, c_dst, c_src = load_rows(c, H, "c_raw")
+        x_raw, x_dst, x_src = load_rows(x, D, "x_raw")
+        xz_raw, xz_dst, xz_src = load_rows(xz_o, H, "xz_raw")
+
+        for g in range(H // K_PASS):
+            k_cols = slice(g * K_PASS, (g + 1) * K_PASS)
+            nc.sync.dma_start(out=h_dst[:, :, k_cols], in_=h_src[:, :, k_cols])
+        nc.sync.dma_start(out=c_dst, in_=c_src)
+        for piece in range(2):
+            k_cols = slice(piece * H, (piece + 1) * H)
+            nc.sync.dma_start(out=x_dst[:, :, k_cols], in_=x_src[:, :, k_cols])
+
+        weight_rows = []
+        for w, k_size in ((w_ho, H), (w_co, H), (w_c, H), (w_i, D)):
+            for g in range(k_size // K_PASS):
+                weight_rows.append(w[g * K_PASS : (g + 1) * K_PASS, :])
+
+        def load_weight_pass(i):
+            raw = w_raw_pool.tile([P, PACK, H], BF16, name="w_raw")
+            nc.sync.dma_start(
+                out=raw[:].rearrange("q (u e) n -> q u e n", u=2),
+                in_=weight_rows[i].rearrange("(u q e) n -> q u e n", u=2, e=2),
+            )
+            return raw
+
+        w_raw = {}
+        for i in range(W_RAW_BUFS):
+            w_raw[i] = load_weight_pass(i)
+            if i == 1:
+                nc.sync.dma_start(out=xz_dst, in_=xz_src)
+
+        ident = keep.tile([P, P], F32, name="ident")
+        make_identity(nc, ident[:])
+
+        table_in = keep.tile([P, 1], F32, name="table_in")
+        table_out = keep.tile([P, 1], F32, name="table_out")
+        nc.vector.memset(table_in[:], 0.0)
+        nc.scalar.activation(out=table_out[:], in_=table_in[:], func=TANH)
+
+        ones = keep.tile([P, P], BF16, name="ones")
+        b_all = keep.tile([P, H], F32, name="b_all")
+        nc.vector.memset(ones[:], 1.0)
+        for half in range(HALVES):
+            n_cols = slice(half * BANK, (half + 1) * BANK)
+            b_bank = psum.tile([P, BANK], F32, name="b_bank", tag="bank")
+            nc.tensor.matmul(out=b_bank[:], lhsT=ones[:], rhs=b_row[:, n_cols], start=True, stop=True)
+            nc.scalar.copy(out=b_all[:, n_cols], in_=b_bank[:])
+
+        act_codes = keep.tile([P, PASSES, B], U32, name="act_codes", align_bytes=64)
+        act_scales = keep.tile([P, PASSES, B], U8, name="act_scales", align_bytes=64)
+        w_codes = keep.tile([P, PASSES, H], U32, name="w_codes", align_bytes=64)
+        w_scales = keep.tile([P, PASSES, H], U8, name="w_scales", align_bytes=64)
+
+        def transpose_pass(words, row_words, g):
+            grouped = act_stage.tile([P, B * PACK], BF16, name="act_grouped", align_bytes=64)
+            grouped_words = grouped[:].bitcast(F32)
+            for pair in range(B_TILES // 2):
+                bank = psum.tile([P, 4, P], F32, name="t_bank", tag="bank")
+                for j in range(4):
+                    t, u = 2 * pair + j // 2, j % 2
+                    first = t * row_words + (2 * g + u) * P
+                    nc.tensor.transpose(bank[:, j, :], words[:, first : first + P], ident[:])
+                copy = nc.vector.tensor_copy if pair == 0 else nc.scalar.copy
+                copy(
+                    out=grouped_words[:, pair * BANK : (pair + 1) * BANK].rearrange(
+                        "q (t r u) -> q t r u", t=2, u=2
+                    ),
+                    in_=bank[:].rearrange("q (t u) r -> q t r u", u=2),
+                )
+            return grouped
+
+        def quantise_activation(i, grouped):
+            nc.vector.quantize_mx(
+                out=act_codes[:, i, :].bitcast(FP8X4), scales=act_scales[:, i, :], in_=grouped[:]
+            )
+
+        sources = []
+        for first, raw, k_size in ((FIRST_H, h_raw, H), (FIRST_C, c_raw, H), (FIRST_X, x_raw, D)):
+            for g in range(k_size // K_PASS):
+                sources.append((first + g, raw[:].bitcast(F32), k_size // 2, g))
+
+        waiting = []
+        for i, words, row_words, g in sources:
+            grouped = transpose_pass(words, row_words, g)
+            fresh = [(i, grouped)]
+            if FIRST_C <= i < FIRST_TANH_C:
+                tanh_grouped = act_stage.tile([P, B * PACK], BF16, name="tanh_grouped", tag="act_grouped", align_bytes=64)
+                nc.scalar.activation(out=tanh_grouped[:], in_=grouped[:], func=TANH)
+                fresh.append((i - FIRST_C + FIRST_TANH_C, tanh_grouped))
+            for item in waiting:
+                quantise_activation(*item)
+            waiting = fresh
+        for item in waiting:
+            quantise_activation(*item)
+
+        gate = keep.tile([P, B_TILES, H], F32, name="gate")
+        xz_view = xz_raw[:].rearrange("p (t n) -> p t n", t=B_TILES)
+
+        def add_bias():
+            for t in range(B_TILES):
+                nc.vector.tensor_tensor(out=gate[:, t, :], in0=xz_view[:, t, :], in1=b_all[:], op=ADD)
+
+        def regroup(i):
+            halves = []
+            for half, copy in ((0, nc.vector.tensor_copy), (1, nc.scalar.copy)):
+                grouped = w_stage.tile([P, BANK, PACK], BF16, name="w_grouped%d" % half, align_bytes=64)
+                copy(
+                    out=grouped[:].rearrange("q (m i) j -> q m j i", i=4),
+                    in_=w_raw[i][:, :, half * BANK : (half + 1) * BANK].rearrange("q j (m i) -> q m j i", i=4),
+                )
+                halves.append(grouped)
+            return halves
+
+        def quantise_weights(i, halves):
+            for half in range(HALVES):
+                n_cols = slice(half * BANK, (half + 1) * BANK)
+                nc.vector.quantize_mx(
+                    out=w_codes[:, i, n_cols].bitcast(FP8X4),
+                    scales=w_scales[:, i, n_cols],
+                    in_=halves[half][:].rearrange("q n j -> q (n j)"),
+                )
+
+        def multiply(i, acc, passes):
+            for half in range(HALVES):
+                n_cols = slice(half * BANK, (half + 1) * BANK)
+                for t in range(B_TILES):
+                    rows = slice(t * P, (t + 1) * P)
+                    nc.tensor.matmul_mx(
+                        out=acc[half, t][:],
+                        lhsT=act_codes[:, i, rows].bitcast(FP8X4),
+                        lhsT_scale=act_scales[:, i, rows],
+                        rhs=w_codes[:, i, n_cols].bitcast(FP8X4),
+                        rhs_scale=w_scales[:, i, n_cols],
+                        start=(i == passes[0]),
+                        stop=(i == passes[-1]),
+                    )
+
+        def open_banks(name):
+            acc = {}
+            for half in range(HALVES):
+                for t in range(B_TILES):
+                    acc[half, t] = psum.tile([P, BANK], F32, name=name, tag="bank")
+            return acc
+
+        out_view = out.rearrange("(p t) n -> p t n", t=B_TILES)
+        acc = None
+        grouped_next = regroup(0)
+        for i in range(PASSES):
+            grouped_now = grouped_next
+            if i + W_RAW_BUFS < PASSES:
+                w_raw[i + W_RAW_BUFS] = load_weight_pass(i + W_RAW_BUFS)
+            if i + 1 < PASSES:
+                grouped_next = regroup(i + 1)
+            quantise_weights(i, grouped_now)
+            if i == 1:
+                add_bias()
+
+            if i == GATE_PASSES[0]:
+                acc = open_banks("o_bank")
+            if i == PROJECTION_PASSES[0]:
+                acc = open_banks("p_bank")
+            multiply(i, acc, GATE_PASSES if i in GATE_PASSES else PROJECTION_PASSES)
+
+            if i == GATE_PASSES[-1]:
+                for half in range(HALVES):
+                    n_cols = slice(half * BANK, (half + 1) * BANK)
+                    for t in range(B_TILES):
+                        nc.vector.tensor_tensor(out=gate[:, t, n_cols], in0=acc[half, t][:], in1=gate[:, t, n_cols], op=ADD)
+                        nc.scalar.activation(out=gate[:, t, n_cols], in_=gate[:, t, n_cols], func=TANH)
+            if i == PROJECTION_PASSES[-1]:
+                for half in range(HALVES):
+                    n_cols = slice(half * BANK, (half + 1) * BANK)
+                    for t in range(B_TILES):
+                        nc.vector.tensor_tensor(out=gate[:, t, n_cols], in0=acc[half, t][:], in1=gate[:, t, n_cols], op=MULT)
+                        nc.sync.dma_start(out=out_view[:, t, n_cols], in_=gate[:, t, n_cols])

@@ -29,6 +29,7 @@ GATE_PASSES = (0, 1, 2, 3)
 PROJECTION_PASSES = (4, 5, 6, 7, 8, 9)
 
 W_RAW_BUFS = 5
+V_COLS = 448
 
 FLOPS = 2 * B * H * (H + H + H + D)
 
@@ -36,8 +37,10 @@ FLOPS = 2 * B * H * (H + H + H + D)
 def tile_residuallstmcell_pb_kernel(tc, x, xz_o, h_prev, c, w_i, w_ho, w_co, w_c, b_o, out):
     nc = tc.nc
     with ExitStack() as ctx:
+        ctx.enter_context(tc.manual_schedule())
         keep = ctx.enter_context(tc.tile_pool(name="keep", bufs=1))
-        act_stage = ctx.enter_context(tc.tile_pool(name="act_stage", bufs=5))
+        act_stage = ctx.enter_context(tc.tile_pool(name="act_stage", bufs=3))
+        tanh_stage = ctx.enter_context(tc.tile_pool(name="tanh_stage", bufs=2))
         w_raw_pool = ctx.enter_context(tc.tile_pool(name="w_raw", bufs=W_RAW_BUFS))
         w_stage = ctx.enter_context(tc.tile_pool(name="w_stage", bufs=3))
         psum = ctx.enter_context(tc.psum_pool(name="psum", bufs=8))
@@ -46,41 +49,38 @@ def tile_residuallstmcell_pb_kernel(tc, x, xz_o, h_prev, c, w_i, w_ho, w_co, w_c
         nc.vector.memset(b_row[:], 0.0)
         nc.sync.dma_start(out=b_row[0:1, :], in_=b_o.rearrange("(o n) -> o n", o=1))
 
-        def load_rows(src, width, name):
-            raw = keep.tile([P, B_TILES * width], BF16, name=name)
-            return raw, raw[:].rearrange("p (t k) -> p t k", t=B_TILES), src.rearrange("(p t) k -> p t k", t=B_TILES)
+        def load_rows(src, raw, pieces):
+            dst = raw[:].rearrange("p (t k) -> p t k", t=B_TILES)
+            rows = src.rearrange("(p t) k -> p t k", t=B_TILES)
+            width = src.shape[1] // pieces
+            for piece in range(pieces):
+                k_cols = slice(piece * width, (piece + 1) * width)
+                nc.sync.dma_start(out=dst[:, :, k_cols], in_=rows[:, :, k_cols])
 
-        h_raw, h_dst, h_src = load_rows(h_prev, H, "h_raw")
-        c_raw, c_dst, c_src = load_rows(c, H, "c_raw")
-        x_raw, x_dst, x_src = load_rows(x, D, "x_raw")
-        xz_raw, xz_dst, xz_src = load_rows(xz_o, H, "xz_raw")
-
-        for g in range(H // K_PASS):
-            k_cols = slice(g * K_PASS, (g + 1) * K_PASS)
-            nc.sync.dma_start(out=h_dst[:, :, k_cols], in_=h_src[:, :, k_cols])
-        nc.sync.dma_start(out=c_dst, in_=c_src)
-        for piece in range(2):
-            k_cols = slice(piece * H, (piece + 1) * H)
-            nc.sync.dma_start(out=x_dst[:, :, k_cols], in_=x_src[:, :, k_cols])
+        c_raw = keep.tile([P, B_TILES * H], BF16, name="c_raw")
+        h_raw = keep.tile([P, B_TILES * H], BF16, name="h_raw")
+        x_raw = keep.tile([P, B_TILES * D], BF16, name="x_raw")
+        xz_raw = keep.tile([P, B_TILES * H], BF16, name="xz_raw")
+        load_rows(c, c_raw, 2)
+        load_rows(h_prev, h_raw, 1)
+        load_rows(x, x_raw, 2)
 
         weight_rows = []
         for w, k_size in ((w_ho, H), (w_co, H), (w_c, H), (w_i, D)):
             for g in range(k_size // K_PASS):
                 weight_rows.append(w[g * K_PASS : (g + 1) * K_PASS, :])
 
+        w_raw = {}
+
         def load_weight_pass(i):
-            raw = w_raw_pool.tile([P, PACK, H], BF16, name="w_raw")
+            w_raw[i] = w_raw_pool.tile([P, PACK, H], BF16, name="w_raw")
             nc.sync.dma_start(
-                out=raw[:].rearrange("q (u e) n -> q u e n", u=2),
+                out=w_raw[i][:].rearrange("q (u e) n -> q u e n", u=2),
                 in_=weight_rows[i].rearrange("(u q e) n -> q u e n", u=2, e=2),
             )
-            return raw
 
-        w_raw = {}
         for i in range(W_RAW_BUFS):
-            w_raw[i] = load_weight_pass(i)
-            if i == 1:
-                nc.sync.dma_start(out=xz_dst, in_=xz_src)
+            load_weight_pass(i)
 
         ident = keep.tile([P, P], F32, name="ident")
         make_identity(nc, ident[:])
@@ -104,7 +104,7 @@ def tile_residuallstmcell_pb_kernel(tc, x, xz_o, h_prev, c, w_i, w_ho, w_co, w_c
         w_codes = keep.tile([P, PASSES, H], U32, name="w_codes", align_bytes=64)
         w_scales = keep.tile([P, PASSES, H], U8, name="w_scales", align_bytes=64)
 
-        def transpose_pass(words, row_words, g):
+        def transpose_pass(words, row_words, g, copy):
             grouped = act_stage.tile([P, B * PACK], BF16, name="act_grouped", align_bytes=64)
             grouped_words = grouped[:].bitcast(F32)
             for pair in range(B_TILES // 2):
@@ -113,7 +113,6 @@ def tile_residuallstmcell_pb_kernel(tc, x, xz_o, h_prev, c, w_i, w_ho, w_co, w_c
                     t, u = 2 * pair + j // 2, j % 2
                     first = t * row_words + (2 * g + u) * P
                     nc.tensor.transpose(bank[:, j, :], words[:, first : first + P], ident[:])
-                copy = nc.vector.tensor_copy if pair == 0 else nc.scalar.copy
                 copy(
                     out=grouped_words[:, pair * BANK : (pair + 1) * BANK].rearrange(
                         "q (t r u) -> q t r u", t=2, u=2
@@ -128,58 +127,59 @@ def tile_residuallstmcell_pb_kernel(tc, x, xz_o, h_prev, c, w_i, w_ho, w_co, w_c
             )
 
         sources = []
-        for first, raw, k_size in ((FIRST_H, h_raw, H), (FIRST_C, c_raw, H), (FIRST_X, x_raw, D)):
+        for first, raw, k_size, copy in (
+            (FIRST_C, c_raw, H, nc.vector.tensor_copy),
+            (FIRST_H, h_raw, H, nc.vector.tensor_copy),
+            (FIRST_X, x_raw, D, nc.scalar.copy),
+        ):
             for g in range(k_size // K_PASS):
-                sources.append((first + g, raw[:].bitcast(F32), k_size // 2, g))
+                sources.append((first + g, raw[:].bitcast(F32), k_size // 2, g, copy))
 
-        waiting = []
-        for i, words, row_words, g in sources:
-            grouped = transpose_pass(words, row_words, g)
-            fresh = [(i, grouped)]
+        tanh_grouped = {}
+        waiting = None
+        for i, words, row_words, g, copy in sources:
+            grouped = transpose_pass(words, row_words, g, copy)
             if FIRST_C <= i < FIRST_TANH_C:
-                tanh_grouped = act_stage.tile([P, B * PACK], BF16, name="tanh_grouped", tag="act_grouped", align_bytes=64)
-                nc.scalar.activation(out=tanh_grouped[:], in_=grouped[:], func=TANH)
-                fresh.append((i - FIRST_C + FIRST_TANH_C, tanh_grouped))
-            for item in waiting:
-                quantise_activation(*item)
-            waiting = fresh
-        for item in waiting:
-            quantise_activation(*item)
+                tanh_grouped[i] = tanh_stage.tile([P, B * PACK], BF16, name="tanh_grouped", align_bytes=64)
+                nc.scalar.activation(out=tanh_grouped[i][:], in_=grouped[:], func=TANH)
+            if waiting is not None:
+                quantise_activation(*waiting)
+            waiting = (i, grouped)
+        quantise_activation(*waiting)
 
-        gate = keep.tile([P, B_TILES, H], F32, name="gate")
-        xz_view = xz_raw[:].rearrange("p (t n) -> p t n", t=B_TILES)
-
-        def add_bias():
-            for t in range(B_TILES):
-                nc.vector.tensor_tensor(out=gate[:, t, :], in0=xz_view[:, t, :], in1=b_all[:], op=ADD)
+        w_grouped = {}
 
         def regroup(i):
-            halves = []
-            for half, copy in ((0, nc.vector.tensor_copy), (1, nc.scalar.copy)):
-                grouped = w_stage.tile([P, BANK, PACK], BF16, name="w_grouped%d" % half, align_bytes=64)
+            w_grouped[i] = w_stage.tile([P, H, PACK], BF16, name="w_grouped", align_bytes=64)
+            for copy, n_cols in ((nc.vector.tensor_copy, slice(0, V_COLS)), (nc.scalar.copy, slice(V_COLS, H))):
                 copy(
-                    out=grouped[:].rearrange("q (m i) j -> q m j i", i=4),
-                    in_=w_raw[i][:, :, half * BANK : (half + 1) * BANK].rearrange("q j (m i) -> q m j i", i=4),
+                    out=w_grouped[i][:, n_cols, :].rearrange("q (m i) j -> q m j i", i=4),
+                    in_=w_raw[i][:, :, n_cols].rearrange("q j (m i) -> q m j i", i=4),
                 )
-                halves.append(grouped)
-            return halves
+            if i + W_RAW_BUFS < PASSES:
+                load_weight_pass(i + W_RAW_BUFS)
 
-        def quantise_weights(i, halves):
+        def quantise_weights(i):
+            nc.vector.quantize_mx(
+                out=w_codes[:, i, :].bitcast(FP8X4),
+                scales=w_scales[:, i, :],
+                in_=w_grouped[i][:].rearrange("q n j -> q (n j)"),
+            )
+
+        def open_banks(name):
+            banks = {}
             for half in range(HALVES):
-                n_cols = slice(half * BANK, (half + 1) * BANK)
-                nc.vector.quantize_mx(
-                    out=w_codes[:, i, n_cols].bitcast(FP8X4),
-                    scales=w_scales[:, i, n_cols],
-                    in_=halves[half][:].rearrange("q n j -> q (n j)"),
-                )
+                for t in range(B_TILES):
+                    banks[half, t] = psum.tile([P, BANK], F32, name=name, tag="bank")
+            return banks
 
-        def multiply(i, acc, passes):
+        def multiply(i, banks, passes):
             for half in range(HALVES):
                 n_cols = slice(half * BANK, (half + 1) * BANK)
                 for t in range(B_TILES):
                     rows = slice(t * P, (t + 1) * P)
                     nc.tensor.matmul_mx(
-                        out=acc[half, t][:],
+                        out=banks[half, t][:],
                         lhsT=act_codes[:, i, rows].bitcast(FP8X4),
                         lhsT_scale=act_scales[:, i, rows],
                         rhs=w_codes[:, i, n_cols].bitcast(FP8X4),
@@ -188,41 +188,41 @@ def tile_residuallstmcell_pb_kernel(tc, x, xz_o, h_prev, c, w_i, w_ho, w_co, w_c
                         stop=(i == passes[-1]),
                     )
 
-        def open_banks(name):
-            acc = {}
-            for half in range(HALVES):
-                for t in range(B_TILES):
-                    acc[half, t] = psum.tile([P, BANK], F32, name=name, tag="bank")
-            return acc
-
+        gate = keep.tile([P, B_TILES, H], F32, name="gate")
+        xz_view = xz_raw[:].rearrange("p (t n) -> p t n", t=B_TILES)
         out_view = out.rearrange("(p t) n -> p t n", t=B_TILES)
-        acc = None
-        grouped_next = regroup(0)
+
+        regroup(0)
+        load_rows(xz_o, xz_raw, 1)
+        for i in range(FIRST_C, FIRST_TANH_C):
+            quantise_activation(i - FIRST_C + FIRST_TANH_C, tanh_grouped[i])
+
+        FIRST_BIAS = PROJECTION_PASSES[1]
+        banks = open_banks("o_bank")
         for i in range(PASSES):
-            grouped_now = grouped_next
-            if i + W_RAW_BUFS < PASSES:
-                w_raw[i + W_RAW_BUFS] = load_weight_pass(i + W_RAW_BUFS)
             if i + 1 < PASSES:
-                grouped_next = regroup(i + 1)
-            quantise_weights(i, grouped_now)
-            if i == 1:
-                add_bias()
+                regroup(i + 1)
+            if FIRST_BIAS < i <= FIRST_BIAS + B_TILES:
+                t = i - FIRST_BIAS - 1
+                nc.scalar.activation(out=gate[:, t, :], in_=gate[:, t, :], func=TANH)
+            quantise_weights(i)
 
-            if i == GATE_PASSES[0]:
-                acc = open_banks("o_bank")
             if i == PROJECTION_PASSES[0]:
-                acc = open_banks("p_bank")
-            multiply(i, acc, GATE_PASSES if i in GATE_PASSES else PROJECTION_PASSES)
+                for half in range(HALVES):
+                    n_cols = slice(half * BANK, (half + 1) * BANK)
+                    for t in range(B_TILES):
+                        nc.vector.tensor_tensor(
+                            out=gate[:, t, n_cols], in0=banks[half, t][:], in1=xz_view[:, t, n_cols], op=ADD
+                        )
+                banks = open_banks("p_bank")
+            multiply(i, banks, GATE_PASSES if i in GATE_PASSES else PROJECTION_PASSES)
 
-            if i == GATE_PASSES[-1]:
-                for half in range(HALVES):
-                    n_cols = slice(half * BANK, (half + 1) * BANK)
-                    for t in range(B_TILES):
-                        nc.vector.tensor_tensor(out=gate[:, t, n_cols], in0=acc[half, t][:], in1=gate[:, t, n_cols], op=ADD)
-                        nc.scalar.activation(out=gate[:, t, n_cols], in_=gate[:, t, n_cols], func=TANH)
-            if i == PROJECTION_PASSES[-1]:
-                for half in range(HALVES):
-                    n_cols = slice(half * BANK, (half + 1) * BANK)
-                    for t in range(B_TILES):
-                        nc.vector.tensor_tensor(out=gate[:, t, n_cols], in0=acc[half, t][:], in1=gate[:, t, n_cols], op=MULT)
-                        nc.sync.dma_start(out=out_view[:, t, n_cols], in_=gate[:, t, n_cols])
+            if FIRST_BIAS <= i < FIRST_BIAS + B_TILES:
+                t = i - FIRST_BIAS
+                nc.vector.tensor_tensor(out=gate[:, t, :], in0=gate[:, t, :], in1=b_all[:], op=ADD)
+
+        for half in range(HALVES):
+            n_cols = slice(half * BANK, (half + 1) * BANK)
+            for t in range(B_TILES):
+                nc.vector.tensor_tensor(out=gate[:, t, n_cols], in0=banks[half, t][:], in1=gate[:, t, n_cols], op=MULT)
+                nc.sync.dma_start(out=out_view[:, t, n_cols], in_=gate[:, t, n_cols])

@@ -29,7 +29,8 @@ GATE_PASSES = (0, 1, 2, 3)
 PROJECTION_PASSES = (4, 5, 6, 7, 8, 9)
 
 W_RAW_BUFS = 5
-V_COLS = 448
+V_COLS_GATE = 512
+V_COLS_PROJECTION = 320
 
 FLOPS = 2 * B * H * (H + H + H + D)
 
@@ -151,7 +152,8 @@ def tile_residuallstmcell_pb_kernel(tc, x, xz_o, h_prev, c, w_i, w_ho, w_co, w_c
 
         def regroup(i):
             w_grouped[i] = w_stage.tile([P, H, PACK], BF16, name="w_grouped", align_bytes=64)
-            for copy, n_cols in ((nc.vector.tensor_copy, slice(0, V_COLS)), (nc.scalar.copy, slice(V_COLS, H))):
+            v_cols = V_COLS_GATE if i in GATE_PASSES else V_COLS_PROJECTION
+            for copy, n_cols in ((nc.vector.tensor_copy, slice(0, v_cols)), (nc.scalar.copy, slice(v_cols, H))):
                 copy(
                     out=w_grouped[i][:, n_cols, :].rearrange("q (m i) j -> q m j i", i=4),
                     in_=w_raw[i][:, :, n_cols].rearrange("q j (m i) -> q m j i", i=4),
@@ -197,12 +199,12 @@ def tile_residuallstmcell_pb_kernel(tc, x, xz_o, h_prev, c, w_i, w_ho, w_co, w_c
         for i in range(FIRST_C, FIRST_TANH_C):
             quantise_activation(i - FIRST_C + FIRST_TANH_C, tanh_grouped[i])
 
-        FIRST_BIAS = PROJECTION_PASSES[1]
+        FIRST_BIAS = PASSES - B_TILES
         banks = open_banks("o_bank")
         for i in range(PASSES):
             if i + 1 < PASSES:
                 regroup(i + 1)
-            if FIRST_BIAS < i <= FIRST_BIAS + B_TILES:
+            if i > FIRST_BIAS:
                 t = i - FIRST_BIAS - 1
                 nc.scalar.activation(out=gate[:, t, :], in_=gate[:, t, :], func=TANH)
             quantise_weights(i)
@@ -217,9 +219,10 @@ def tile_residuallstmcell_pb_kernel(tc, x, xz_o, h_prev, c, w_i, w_ho, w_co, w_c
                 banks = open_banks("p_bank")
             multiply(i, banks, GATE_PASSES if i in GATE_PASSES else PROJECTION_PASSES)
 
-            if FIRST_BIAS <= i < FIRST_BIAS + B_TILES:
+            if i >= FIRST_BIAS:
                 t = i - FIRST_BIAS
                 nc.vector.tensor_tensor(out=gate[:, t, :], in0=gate[:, t, :], in1=b_all[:], op=ADD)
+        nc.scalar.activation(out=gate[:, B_TILES - 1, :], in_=gate[:, B_TILES - 1, :], func=TANH)
 
         for half in range(HALVES):
             n_cols = slice(half * BANK, (half + 1) * BANK)

@@ -38,7 +38,6 @@ FLOPS = 2 * B * H * (H + H + H + D)
 def tile_residuallstmcell_pb_kernel(tc, x, xz_o, h_prev, c, w_i, w_ho, w_co, w_c, b_o, out):
     nc = tc.nc
     with ExitStack() as ctx:
-        ctx.enter_context(tc.manual_schedule())
         keep = ctx.enter_context(tc.tile_pool(name="keep", bufs=1))
         act_stage = ctx.enter_context(tc.tile_pool(name="act_stage", bufs=3))
         tanh_stage = ctx.enter_context(tc.tile_pool(name="tanh_stage", bufs=2))

@@ -27,10 +27,13 @@ FIRST_X = 6
 PASSES = 10
 GATE_PASSES = (0, 1, 2, 3)
 PROJECTION_PASSES = (4, 5, 6, 7, 8, 9)
+LAST_PAIR = (8, 9)
 
-W_RAW_BUFS = 5
-V_COLS_GATE = 512
-V_COLS_PROJECTION = 320
+PE_COLS = (512, 512, 512, 512, 512, 512, 512, 0, 0, 0)
+V_COLS = (288, 288, 288, 288, 288, 288, 288, 544, 544, 544)
+PE_CHUNK = 256
+
+RAW_BUFS = 11
 
 FLOPS = 2 * B * H * (H + H + H + D)
 
@@ -39,31 +42,32 @@ def tile_residuallstmcell_pb_kernel(tc, x, xz_o, h_prev, c, w_i, w_ho, w_co, w_c
     nc = tc.nc
     with ExitStack() as ctx:
         keep = ctx.enter_context(tc.tile_pool(name="keep", bufs=1))
+        raw_pool = ctx.enter_context(tc.tile_pool(name="raw_pool", bufs=RAW_BUFS))
         act_stage = ctx.enter_context(tc.tile_pool(name="act_stage", bufs=3))
-        tanh_stage = ctx.enter_context(tc.tile_pool(name="tanh_stage", bufs=2))
-        w_raw_pool = ctx.enter_context(tc.tile_pool(name="w_raw", bufs=W_RAW_BUFS))
+        tanh_stage = ctx.enter_context(tc.tile_pool(name="tanh_stage", bufs=4))
         w_stage = ctx.enter_context(tc.tile_pool(name="w_stage", bufs=3))
-        psum = ctx.enter_context(tc.psum_pool(name="psum", bufs=8))
+        psum_x = ctx.enter_context(tc.psum_pool(name="psum_x", bufs=4))
+        psum_p = ctx.enter_context(tc.psum_pool(name="psum_p", bufs=4))
 
         b_row = keep.tile([P, H], BF16, name="b_row")
         nc.vector.memset(b_row[:], 0.0)
         nc.sync.dma_start(out=b_row[0:1, :], in_=b_o.rearrange("(o n) -> o n", o=1))
 
-        def load_rows(src, raw, pieces):
-            dst = raw[:].rearrange("p (t k) -> p t k", t=B_TILES)
+        def load_rows(src, t_first, t_count, pieces):
+            k_size = src.shape[1]
+            raw = raw_pool.tile([P, t_count, k_size], BF16, name="raw", tag="raw")
             rows = src.rearrange("(p t) k -> p t k", t=B_TILES)
-            width = src.shape[1] // pieces
+            step = t_count // pieces
             for piece in range(pieces):
-                k_cols = slice(piece * width, (piece + 1) * width)
-                nc.sync.dma_start(out=dst[:, :, k_cols], in_=rows[:, :, k_cols])
+                lo = piece * step
+                nc.sync.dma_start(
+                    out=raw[:, lo : lo + step, :], in_=rows[:, t_first + lo : t_first + lo + step, :]
+                )
+            return raw
 
-        c_raw = keep.tile([P, B_TILES * H], BF16, name="c_raw")
-        h_raw = keep.tile([P, B_TILES * H], BF16, name="h_raw")
-        x_raw = keep.tile([P, B_TILES * D], BF16, name="x_raw")
-        xz_raw = keep.tile([P, B_TILES * H], BF16, name="xz_raw")
-        load_rows(c, c_raw, 2)
-        load_rows(h_prev, h_raw, 1)
-        load_rows(x, x_raw, 2)
+        c_raw = load_rows(c, 0, B_TILES, 4)
+        h_raw = load_rows(h_prev, 0, B_TILES, 2)
+        x_raw = [load_rows(x, 0, 2, 2), load_rows(x, 2, 2, 2)]
 
         weight_rows = []
         for w, k_size in ((w_ho, H), (w_co, H), (w_c, H), (w_i, D)):
@@ -73,17 +77,22 @@ def tile_residuallstmcell_pb_kernel(tc, x, xz_o, h_prev, c, w_i, w_ho, w_co, w_c
         w_raw = {}
 
         def load_weight_pass(i):
-            w_raw[i] = w_raw_pool.tile([P, PACK, H], BF16, name="w_raw")
+            w_raw[i] = raw_pool.tile([P, PACK, H], BF16, name="raw", tag="raw")
             nc.sync.dma_start(
                 out=w_raw[i][:].rearrange("q (u e) n -> q u e n", u=2),
                 in_=weight_rows[i].rearrange("(u q e) n -> q u e n", u=2, e=2),
             )
 
-        for i in range(W_RAW_BUFS):
+        load_weight_pass(0)
+        load_weight_pass(1)
+        xz_raw = load_rows(xz_o, 0, B_TILES, 1)
+        for i in range(2, PASSES):
             load_weight_pass(i)
 
         ident = keep.tile([P, P], F32, name="ident")
         make_identity(nc, ident[:])
+        ident_bf = keep.tile([P, P], BF16, name="ident_bf")
+        nc.vector.tensor_copy(out=ident_bf[:], in_=ident[:])
 
         table_in = keep.tile([P, 1], F32, name="table_in")
         table_out = keep.tile([P, 1], F32, name="table_out")
@@ -95,136 +104,174 @@ def tile_residuallstmcell_pb_kernel(tc, x, xz_o, h_prev, c, w_i, w_ho, w_co, w_c
         nc.vector.memset(ones[:], 1.0)
         for half in range(HALVES):
             n_cols = slice(half * BANK, (half + 1) * BANK)
-            b_bank = psum.tile([P, BANK], F32, name="b_bank", tag="bank")
+            b_bank = psum_p.tile([P, BANK], F32, name="b_bank", tag="p")
             nc.tensor.matmul(out=b_bank[:], lhsT=ones[:], rhs=b_row[:, n_cols], start=True, stop=True)
             nc.scalar.copy(out=b_all[:, n_cols], in_=b_bank[:])
 
-        act_codes = keep.tile([P, PASSES, B], U32, name="act_codes", align_bytes=64)
-        act_scales = keep.tile([P, PASSES, B], U8, name="act_scales", align_bytes=64)
+        act_codes = keep.tile([P, B_TILES, PASSES, P], U32, name="act_codes", align_bytes=64)
+        act_scales = keep.tile([P, B_TILES, PASSES, P], U8, name="act_scales", align_bytes=64)
         w_codes = keep.tile([P, PASSES, H], U32, name="w_codes", align_bytes=64)
         w_scales = keep.tile([P, PASSES, H], U8, name="w_scales", align_bytes=64)
 
-        def transpose_pass(words, row_words, g, copy):
-            grouped = act_stage.tile([P, B * PACK], BF16, name="act_grouped", align_bytes=64)
-            grouped_words = grouped[:].bitcast(F32)
-            for pair in range(B_TILES // 2):
-                bank = psum.tile([P, 4, P], F32, name="t_bank", tag="bank")
+        def lay_out(words, groups, grouped, copy, pool, tag):
+            grouped_words = grouped.bitcast(F32)
+            for pair in range(groups // 2):
+                bank = pool.tile([P, 4, P], F32, name="t_bank", tag=tag)
                 for j in range(4):
-                    t, u = 2 * pair + j // 2, j % 2
-                    first = t * row_words + (2 * g + u) * P
+                    first = (4 * pair + j) * P
                     nc.tensor.transpose(bank[:, j, :], words[:, first : first + P], ident[:])
                 copy(
                     out=grouped_words[:, pair * BANK : (pair + 1) * BANK].rearrange(
-                        "q (t r u) -> q t r u", t=2, u=2
+                        "q (g r u) -> q g r u", g=2, u=2
                     ),
-                    in_=bank[:].rearrange("q (t u) r -> q t r u", u=2),
+                    in_=bank[:].rearrange("q (g u) r -> q g r u", u=2),
                 )
-            return grouped
 
-        def quantise_activation(i, grouped):
+        def quantise_activation(t, first, count, grouped):
             nc.vector.quantize_mx(
-                out=act_codes[:, i, :].bitcast(FP8X4), scales=act_scales[:, i, :], in_=grouped[:]
+                out=act_codes[:, t, first : first + count, :].rearrange("q g r -> q (g r)").bitcast(FP8X4),
+                scales=act_scales[:, t, first : first + count, :].rearrange("q g r -> q (g r)"),
+                in_=grouped,
             )
 
-        sources = []
-        for first, raw, k_size, copy in (
-            (FIRST_C, c_raw, H, nc.vector.tensor_copy),
-            (FIRST_H, h_raw, H, nc.vector.tensor_copy),
-            (FIRST_X, x_raw, D, nc.scalar.copy),
-        ):
-            for g in range(k_size // K_PASS):
-                sources.append((first + g, raw[:].bitcast(F32), k_size // 2, g, copy))
-
         tanh_grouped = {}
-        waiting = None
-        for i, words, row_words, g, copy in sources:
-            grouped = transpose_pass(words, row_words, g, copy)
-            if FIRST_C <= i < FIRST_TANH_C:
-                tanh_grouped[i] = tanh_stage.tile([P, B * PACK], BF16, name="tanh_grouped", align_bytes=64)
-                nc.scalar.activation(out=tanh_grouped[i][:], in_=grouped[:], func=TANH)
-            if waiting is not None:
-                quantise_activation(*waiting)
-            waiting = (i, grouped)
-        quantise_activation(*waiting)
+        waiting = []
+
+        def flush(keep_back):
+            while len(waiting) > keep_back:
+                quantise_activation(*waiting.pop(0))
+
+        for t in range(B_TILES):
+            grouped = act_stage.tile([P, H], BF16, name="c_grouped", tag="act", align_bytes=64)
+            lay_out(c_raw[:, t, :].bitcast(F32), 2, grouped[:], nc.vector.tensor_copy, psum_x, "x")
+            tanh_grouped[t] = tanh_stage.tile([P, H], BF16, name="tanh_grouped", align_bytes=64)
+            nc.scalar.activation(out=tanh_grouped[t][:], in_=grouped[:], func=TANH)
+            waiting.append((t, FIRST_C, 2, grouped[:]))
+            flush(1)
+        for t in range(B_TILES):
+            grouped = act_stage.tile([P, H], BF16, name="h_grouped", tag="act", align_bytes=64)
+            lay_out(h_raw[:, t, :].bitcast(F32), 2, grouped[:], nc.vector.tensor_copy, psum_x, "x")
+            waiting.append((t, FIRST_H, 2, grouped[:]))
+            flush(1)
+            waiting.append((t, FIRST_TANH_C, 2, tanh_grouped[t][:]))
+        for t in range(B_TILES):
+            grouped = act_stage.tile([P, D], BF16, name="x_grouped", tag="act", align_bytes=64)
+            lay_out(x_raw[t // 2][:, t % 2, :].bitcast(F32), 4, grouped[:], nc.scalar.copy, psum_p, "p")
+            waiting.append((t, FIRST_X, 4, grouped[:]))
+            flush(1)
 
         w_grouped = {}
 
-        def regroup(i):
-            w_grouped[i] = w_stage.tile([P, H, PACK], BF16, name="w_grouped", align_bytes=64)
-            v_cols = V_COLS_GATE if i in GATE_PASSES else V_COLS_PROJECTION
-            for copy, n_cols in ((nc.vector.tensor_copy, slice(0, v_cols)), (nc.scalar.copy, slice(v_cols, H))):
+        def regroup(i, n_lo, n_hi, pe_cols, v_cols):
+            if i not in w_grouped:
+                w_grouped[i] = w_stage.tile([P, H, PACK], BF16, name="w_grouped", align_bytes=64)
+            for n0 in range(n_lo, n_lo + pe_cols, PE_CHUNK):
+                bank = psum_x.tile([P, PE_CHUNK, PACK], BF16, name="w_bank", tag="x")
+                for part in range(2):
+                    lo = part * (PE_CHUNK // 2)
+                    cols = slice(n0 + lo, n0 + lo + PE_CHUNK // 2)
+                    nc.tensor.matmul(
+                        out=bank[:, lo : lo + PE_CHUNK // 2, :].rearrange("q n j -> q (n j)"),
+                        lhsT=ident_bf[:],
+                        rhs=w_raw[i][:, :, cols].rearrange("q j n -> q n j"),
+                        start=True,
+                        stop=True,
+                    )
+                nc.scalar.copy(out=w_grouped[i][:, n0 : n0 + PE_CHUNK, :], in_=bank[:])
+            v_lo = n_lo + pe_cols
+            s_lo = v_lo + v_cols
+            for copy, cols in ((nc.vector.tensor_copy, slice(v_lo, s_lo)), (nc.scalar.copy, slice(s_lo, n_hi))):
                 copy(
-                    out=w_grouped[i][:, n_cols, :].rearrange("q (m i) j -> q m j i", i=4),
-                    in_=w_raw[i][:, :, n_cols].rearrange("q j (m i) -> q m j i", i=4),
+                    out=w_grouped[i][:, cols, :].rearrange("q (m i) j -> q m j i", i=4),
+                    in_=w_raw[i][:, :, cols].rearrange("q j (m i) -> q m j i", i=4),
                 )
-            if i + W_RAW_BUFS < PASSES:
-                load_weight_pass(i + W_RAW_BUFS)
 
-        def quantise_weights(i):
+        def quantise_weights(i, n_lo, n_hi):
             nc.vector.quantize_mx(
-                out=w_codes[:, i, :].bitcast(FP8X4),
-                scales=w_scales[:, i, :],
-                in_=w_grouped[i][:].rearrange("q n j -> q (n j)"),
+                out=w_codes[:, i, n_lo:n_hi].bitcast(FP8X4),
+                scales=w_scales[:, i, n_lo:n_hi],
+                in_=w_grouped[i][:, n_lo:n_hi, :].rearrange("q n j -> q (n j)"),
             )
 
-        def open_banks(name):
-            banks = {}
-            for half in range(HALVES):
-                for t in range(B_TILES):
-                    banks[half, t] = psum.tile([P, BANK], F32, name=name, tag="bank")
-            return banks
-
-        def multiply(i, banks, passes):
-            for half in range(HALVES):
-                n_cols = slice(half * BANK, (half + 1) * BANK)
-                for t in range(B_TILES):
-                    rows = slice(t * P, (t + 1) * P)
-                    nc.tensor.matmul_mx(
-                        out=banks[half, t][:],
-                        lhsT=act_codes[:, i, rows].bitcast(FP8X4),
-                        lhsT_scale=act_scales[:, i, rows],
-                        rhs=w_codes[:, i, n_cols].bitcast(FP8X4),
-                        rhs_scale=w_scales[:, i, n_cols],
-                        start=(i == passes[0]),
-                        stop=(i == passes[-1]),
-                    )
+        def multiply(i, half, t, bank, passes):
+            n_cols = slice(half * BANK, (half + 1) * BANK)
+            nc.tensor.matmul_mx(
+                out=bank[:],
+                lhsT=act_codes[:, t, i, :].bitcast(FP8X4),
+                lhsT_scale=act_scales[:, t, i, :],
+                rhs=w_codes[:, i, n_cols].bitcast(FP8X4),
+                rhs_scale=w_scales[:, i, n_cols],
+                start=(i == passes[0]),
+                stop=(i == passes[-1]),
+            )
 
         gate = keep.tile([P, B_TILES, H], F32, name="gate")
-        xz_view = xz_raw[:].rearrange("p (t n) -> p t n", t=B_TILES)
         out_view = out.rearrange("(p t) n -> p t n", t=B_TILES)
 
-        regroup(0)
-        load_rows(xz_o, xz_raw, 1)
-        for i in range(FIRST_C, FIRST_TANH_C):
-            quantise_activation(i - FIRST_C + FIRST_TANH_C, tanh_grouped[i])
+        def leave_gate_bank(half, t, bank):
+            n_cols = slice(half * BANK, (half + 1) * BANK)
+            nc.vector.tensor_tensor(out=gate[:, t, n_cols], in0=bank[:], in1=gate[:, t, n_cols], op=ADD)
+            nc.scalar.activation(out=gate[:, t, n_cols], in_=gate[:, t, n_cols], func=TANH)
 
-        FIRST_BIAS = PASSES - B_TILES
-        banks = open_banks("o_bank")
-        for i in range(PASSES):
-            if i + 1 < PASSES:
-                regroup(i + 1)
-            if i > FIRST_BIAS:
-                t = i - FIRST_BIAS - 1
-                nc.scalar.activation(out=gate[:, t, :], in_=gate[:, t, :], func=TANH)
-            quantise_weights(i)
+        steps = [(i, 0, H) for i in range(PASSES) if i not in LAST_PAIR]
+        for half in range(HALVES):
+            for i in LAST_PAIR:
+                steps.append((i, half * BANK, (half + 1) * BANK))
+
+        def regroup_step(s):
+            i, n_lo, n_hi = steps[s]
+            share = (n_hi - n_lo) / H
+            regroup(i, n_lo, n_hi, int(PE_COLS[i] * share), int(V_COLS[i] * share))
+
+        o_banks = {}
+        p_banks = {}
+        regroup_step(0)
+        flush(0)
+        for s in range(len(steps)):
+            i, n_lo, n_hi = steps[s]
+            if s + 1 < len(steps):
+                regroup_step(s + 1)
+            if i < B_TILES:
+                nc.vector.tensor_tensor(out=gate[:, i, :], in0=xz_raw[:, i, :], in1=b_all[:], op=ADD)
+            quantise_weights(i, n_lo, n_hi)
+
+            if i in GATE_PASSES:
+                if i == GATE_PASSES[0]:
+                    for t in range(B_TILES):
+                        o_banks[t] = psum_p.tile([P, BANK], F32, name="o_bank", tag="p")
+                for t in range(B_TILES):
+                    multiply(i, 0, t, o_banks[t], GATE_PASSES)
+                if i == GATE_PASSES[-1]:
+                    for t in range(B_TILES):
+                        leave_gate_bank(0, t, o_banks[t])
+                continue
 
             if i == PROJECTION_PASSES[0]:
-                for half in range(HALVES):
-                    n_cols = slice(half * BANK, (half + 1) * BANK)
-                    for t in range(B_TILES):
-                        nc.vector.tensor_tensor(
-                            out=gate[:, t, n_cols], in0=banks[half, t][:], in1=xz_view[:, t, n_cols], op=ADD
-                        )
-                banks = open_banks("p_bank")
-            multiply(i, banks, GATE_PASSES if i in GATE_PASSES else PROJECTION_PASSES)
+                for t in range(B_TILES):
+                    bank = psum_x.tile([P, BANK], F32, name="o_late", tag="x")
+                    for k in GATE_PASSES:
+                        multiply(k, 1, t, bank, GATE_PASSES)
+                    leave_gate_bank(1, t, bank)
+                for t in range(B_TILES):
+                    p_banks[0, t] = psum_p.tile([P, BANK], F32, name="p_bank", tag="p")
+            if n_lo == 0:
+                for t in range(B_TILES):
+                    multiply(i, 0, t, p_banks[0, t], PROJECTION_PASSES)
+            if i == LAST_PAIR[0] - 1:
+                for t in range(B_TILES):
+                    p_banks[1, t] = psum_x.tile([P, BANK], F32, name="p_late", tag="x")
+                    for k in PROJECTION_PASSES:
+                        if k not in LAST_PAIR:
+                            multiply(k, 1, t, p_banks[1, t], PROJECTION_PASSES)
+            if n_lo == BANK:
+                for t in range(B_TILES):
+                    multiply(i, 1, t, p_banks[1, t], PROJECTION_PASSES)
 
-            if i >= FIRST_BIAS:
-                t = i - FIRST_BIAS
-                nc.vector.tensor_tensor(out=gate[:, t, :], in0=gate[:, t, :], in1=b_all[:], op=ADD)
-        nc.scalar.activation(out=gate[:, B_TILES - 1, :], in_=gate[:, B_TILES - 1, :], func=TANH)
-
-        for half in range(HALVES):
-            n_cols = slice(half * BANK, (half + 1) * BANK)
-            for t in range(B_TILES):
-                nc.vector.tensor_tensor(out=gate[:, t, n_cols], in0=banks[half, t][:], in1=gate[:, t, n_cols], op=MULT)
-                nc.sync.dma_start(out=out_view[:, t, n_cols], in_=gate[:, t, n_cols])
+            if i == LAST_PAIR[-1]:
+                half = n_lo // BANK
+                n_cols = slice(n_lo, n_hi)
+                for t in range(B_TILES):
+                    nc.vector.tensor_tensor(
+                        out=gate[:, t, n_cols], in0=p_banks[half, t][:], in1=gate[:, t, n_cols], op=MULT
+                    )
+                    nc.sync.dma_start(out=out_view[:, t, n_cols], in_=gate[:, t, n_cols])

@@ -20,8 +20,8 @@ B_TILES = B // P
 BANK = 512
 HALVES = H // BANK
 
-FIRST_H = 0
-FIRST_C = 2
+FIRST_C = 0
+FIRST_H = 2
 FIRST_TANH_C = 4
 FIRST_X = 6
 PASSES = 10
@@ -29,11 +29,13 @@ GATE_PASSES = (0, 1, 2, 3)
 PROJECTION_PASSES = (4, 5, 6, 7, 8, 9)
 LAST_PAIR = (8, 9)
 
-PE_COLS = (512, 512, 512, 512, 512, 512, 512, 0, 0, 0)
-V_COLS = (288, 288, 288, 288, 288, 288, 288, 544, 544, 544)
+PE_COLS = (512, 512, 512, 512, 512, 512, 0, 0, 0, 0)
+V_COLS = (512, 448, 192, 192, 128, 128, 448, 448, 512, 512)
 PE_CHUNK = 256
 
 RAW_BUFS = 11
+G_BANKS = 2
+X_BANKS = 6
 
 FLOPS = 2 * B * H * (H + H + H + D)
 
@@ -41,17 +43,14 @@ FLOPS = 2 * B * H * (H + H + H + D)
 def tile_residuallstmcell_pb_kernel(tc, x, xz_o, h_prev, c, w_i, w_ho, w_co, w_c, b_o, out):
     nc = tc.nc
     with ExitStack() as ctx:
+        ctx.enter_context(tc.manual_schedule())
         keep = ctx.enter_context(tc.tile_pool(name="keep", bufs=1))
         raw_pool = ctx.enter_context(tc.tile_pool(name="raw_pool", bufs=RAW_BUFS))
         act_stage = ctx.enter_context(tc.tile_pool(name="act_stage", bufs=3))
         tanh_stage = ctx.enter_context(tc.tile_pool(name="tanh_stage", bufs=4))
-        w_stage = ctx.enter_context(tc.tile_pool(name="w_stage", bufs=3))
-        psum_x = ctx.enter_context(tc.psum_pool(name="psum_x", bufs=4))
-        psum_p = ctx.enter_context(tc.psum_pool(name="psum_p", bufs=4))
-
-        b_row = keep.tile([P, H], BF16, name="b_row")
-        nc.vector.memset(b_row[:], 0.0)
-        nc.sync.dma_start(out=b_row[0:1, :], in_=b_o.rearrange("(o n) -> o n", o=1))
+        w_stage = ctx.enter_context(tc.tile_pool(name="w_stage", bufs=4))
+        psum_x = ctx.enter_context(tc.psum_pool(name="psum_x", bufs=X_BANKS))
+        psum_g = ctx.enter_context(tc.psum_pool(name="psum_g", bufs=G_BANKS))
 
         def load_rows(src, t_first, t_count, pieces):
             k_size = src.shape[1]
@@ -65,12 +64,8 @@ def tile_residuallstmcell_pb_kernel(tc, x, xz_o, h_prev, c, w_i, w_ho, w_co, w_c
                 )
             return raw
 
-        c_raw = load_rows(c, 0, B_TILES, 4)
-        h_raw = load_rows(h_prev, 0, B_TILES, 2)
-        x_raw = [load_rows(x, 0, 2, 2), load_rows(x, 2, 2, 2)]
-
         weight_rows = []
-        for w, k_size in ((w_ho, H), (w_co, H), (w_c, H), (w_i, D)):
+        for w, k_size in ((w_co, H), (w_ho, H), (w_c, H), (w_i, D)):
             for g in range(k_size // K_PASS):
                 weight_rows.append(w[g * K_PASS : (g + 1) * K_PASS, :])
 
@@ -83,10 +78,19 @@ def tile_residuallstmcell_pb_kernel(tc, x, xz_o, h_prev, c, w_i, w_ho, w_co, w_c
                 in_=weight_rows[i].rearrange("(u q e) n -> q u e n", u=2, e=2),
             )
 
+        b_row = keep.tile([P, H], BF16, name="b_row")
+        nc.vector.memset(b_row[:], 0.0)
+
+        c_raw = load_rows(c, 0, B_TILES, 4)
         load_weight_pass(0)
         load_weight_pass(1)
+        nc.sync.dma_start(out=b_row[0:1, :], in_=b_o.rearrange("(o n) -> o n", o=1))
+        h_raw = load_rows(h_prev, 0, B_TILES, 2)
+        load_weight_pass(2)
+        load_weight_pass(3)
         xz_raw = load_rows(xz_o, 0, B_TILES, 1)
-        for i in range(2, PASSES):
+        x_raw = [load_rows(x, 0, 2, 2), load_rows(x, 2, 2, 2)]
+        for i in range(4, PASSES):
             load_weight_pass(i)
 
         ident = keep.tile([P, P], F32, name="ident")
@@ -102,11 +106,13 @@ def tile_residuallstmcell_pb_kernel(tc, x, xz_o, h_prev, c, w_i, w_ho, w_co, w_c
         ones = keep.tile([P, P], BF16, name="ones")
         b_all = keep.tile([P, H], F32, name="b_all")
         nc.vector.memset(ones[:], 1.0)
-        for half in range(HALVES):
-            n_cols = slice(half * BANK, (half + 1) * BANK)
-            b_bank = psum_p.tile([P, BANK], F32, name="b_bank", tag="p")
-            nc.tensor.matmul(out=b_bank[:], lhsT=ones[:], rhs=b_row[:, n_cols], start=True, stop=True)
-            nc.scalar.copy(out=b_all[:, n_cols], in_=b_bank[:])
+
+        def spread_bias():
+            for half in range(HALVES):
+                n_cols = slice(half * BANK, (half + 1) * BANK)
+                b_bank = psum_x.tile([P, BANK], F32, name="b_bank", tag="x")
+                nc.tensor.matmul(out=b_bank[:], lhsT=ones[:], rhs=b_row[:, n_cols], start=True, stop=True)
+                nc.scalar.copy(out=b_all[:, n_cols], in_=b_bank[:])
 
         act_codes = keep.tile([P, B_TILES, PASSES, P], U32, name="act_codes", align_bytes=64)
         act_scales = keep.tile([P, B_TILES, PASSES, P], U8, name="act_scales", align_bytes=64)
@@ -134,35 +140,14 @@ def tile_residuallstmcell_pb_kernel(tc, x, xz_o, h_prev, c, w_i, w_ho, w_co, w_c
                 in_=grouped,
             )
 
-        tanh_grouped = {}
-        waiting = []
-
-        def flush(keep_back):
-            while len(waiting) > keep_back:
-                quantise_activation(*waiting.pop(0))
-
-        for t in range(B_TILES):
-            grouped = act_stage.tile([P, H], BF16, name="c_grouped", tag="act", align_bytes=64)
-            lay_out(c_raw[:, t, :].bitcast(F32), 2, grouped[:], nc.vector.tensor_copy, psum_x, "x")
-            tanh_grouped[t] = tanh_stage.tile([P, H], BF16, name="tanh_grouped", align_bytes=64)
-            nc.scalar.activation(out=tanh_grouped[t][:], in_=grouped[:], func=TANH)
-            waiting.append((t, FIRST_C, 2, grouped[:]))
-            flush(1)
-        for t in range(B_TILES):
-            grouped = act_stage.tile([P, H], BF16, name="h_grouped", tag="act", align_bytes=64)
-            lay_out(h_raw[:, t, :].bitcast(F32), 2, grouped[:], nc.vector.tensor_copy, psum_x, "x")
-            waiting.append((t, FIRST_H, 2, grouped[:]))
-            flush(1)
-            waiting.append((t, FIRST_TANH_C, 2, tanh_grouped[t][:]))
-        for t in range(B_TILES):
-            grouped = act_stage.tile([P, D], BF16, name="x_grouped", tag="act", align_bytes=64)
-            lay_out(x_raw[t // 2][:, t % 2, :].bitcast(F32), 4, grouped[:], nc.scalar.copy, psum_p, "p")
-            waiting.append((t, FIRST_X, 4, grouped[:]))
-            flush(1)
-
         w_grouped = {}
 
-        def regroup(i, n_lo, n_hi, pe_cols, v_cols):
+        def regroup(i, n_lo, n_hi):
+            regroup_tensor(i, n_lo, n_hi)
+            regroup_copies(i, n_lo, n_hi)
+
+        def regroup_tensor(i, n_lo, n_hi):
+            pe_cols = PE_COLS[i] * (n_hi - n_lo) // H
             if i not in w_grouped:
                 w_grouped[i] = w_stage.tile([P, H, PACK], BF16, name="w_grouped", align_bytes=64)
             for n0 in range(n_lo, n_lo + pe_cols, PE_CHUNK):
@@ -178,9 +163,17 @@ def tile_residuallstmcell_pb_kernel(tc, x, xz_o, h_prev, c, w_i, w_ho, w_co, w_c
                         stop=True,
                     )
                 nc.scalar.copy(out=w_grouped[i][:, n0 : n0 + PE_CHUNK, :], in_=bank[:])
+
+        def regroup_copies(i, n_lo, n_hi):
+            pe_cols = PE_COLS[i] * (n_hi - n_lo) // H
+            v_cols = V_COLS[i] * (n_hi - n_lo) // H
+            if i not in w_grouped:
+                w_grouped[i] = w_stage.tile([P, H, PACK], BF16, name="w_grouped", align_bytes=64)
             v_lo = n_lo + pe_cols
             s_lo = v_lo + v_cols
             for copy, cols in ((nc.vector.tensor_copy, slice(v_lo, s_lo)), (nc.scalar.copy, slice(s_lo, n_hi))):
+                if cols.start == cols.stop:
+                    continue
                 copy(
                     out=w_grouped[i][:, cols, :].rearrange("q (m i) j -> q m j i", i=4),
                     in_=w_raw[i][:, :, cols].rearrange("q j (m i) -> q m j i", i=4),
@@ -193,7 +186,8 @@ def tile_residuallstmcell_pb_kernel(tc, x, xz_o, h_prev, c, w_i, w_ho, w_co, w_c
                 in_=w_grouped[i][:, n_lo:n_hi, :].rearrange("q n j -> q (n j)"),
             )
 
-        def multiply(i, half, t, bank, passes):
+        def multiply(i, k, bank, passes):
+            half, t = divmod(k, B_TILES)
             n_cols = slice(half * BANK, (half + 1) * BANK)
             nc.tensor.matmul_mx(
                 out=bank[:],
@@ -207,71 +201,165 @@ def tile_residuallstmcell_pb_kernel(tc, x, xz_o, h_prev, c, w_i, w_ho, w_co, w_c
 
         gate = keep.tile([P, B_TILES, H], F32, name="gate")
         out_view = out.rearrange("(p t) n -> p t n", t=B_TILES)
-
-        def leave_gate_bank(half, t, bank):
-            n_cols = slice(half * BANK, (half + 1) * BANK)
-            nc.vector.tensor_tensor(out=gate[:, t, n_cols], in0=bank[:], in1=gate[:, t, n_cols], op=ADD)
-            nc.scalar.activation(out=gate[:, t, n_cols], in_=gate[:, t, n_cols], func=TANH)
-
-        steps = [(i, 0, H) for i in range(PASSES) if i not in LAST_PAIR]
-        for half in range(HALVES):
-            for i in LAST_PAIR:
-                steps.append((i, half * BANK, (half + 1) * BANK))
-
-        def regroup_step(s):
-            i, n_lo, n_hi = steps[s]
-            share = (n_hi - n_lo) / H
-            regroup(i, n_lo, n_hi, int(PE_COLS[i] * share), int(V_COLS[i] * share))
-
+        TILES = HALVES * B_TILES
         o_banks = {}
         p_banks = {}
-        regroup_step(0)
-        flush(0)
-        for s in range(len(steps)):
-            i, n_lo, n_hi = steps[s]
-            if s + 1 < len(steps):
-                regroup_step(s + 1)
-            if i < B_TILES:
-                nc.vector.tensor_tensor(out=gate[:, i, :], in0=xz_raw[:, i, :], in1=b_all[:], op=ADD)
-            quantise_weights(i, n_lo, n_hi)
 
-            if i in GATE_PASSES:
-                if i == GATE_PASSES[0]:
-                    for t in range(B_TILES):
-                        o_banks[t] = psum_p.tile([P, BANK], F32, name="o_bank", tag="p")
-                for t in range(B_TILES):
-                    multiply(i, 0, t, o_banks[t], GATE_PASSES)
-                if i == GATE_PASSES[-1]:
-                    for t in range(B_TILES):
-                        leave_gate_bank(0, t, o_banks[t])
-                continue
+        def gate_view(k):
+            half, t = divmod(k, B_TILES)
+            return gate[:, t, half * BANK : (half + 1) * BANK]
 
-            if i == PROJECTION_PASSES[0]:
-                for t in range(B_TILES):
-                    bank = psum_x.tile([P, BANK], F32, name="o_late", tag="x")
-                    for k in GATE_PASSES:
-                        multiply(k, 1, t, bank, GATE_PASSES)
-                    leave_gate_bank(1, t, bank)
-                for t in range(B_TILES):
-                    p_banks[0, t] = psum_p.tile([P, BANK], F32, name="p_bank", tag="p")
-            if n_lo == 0:
-                for t in range(B_TILES):
-                    multiply(i, 0, t, p_banks[0, t], PROJECTION_PASSES)
-            if i == LAST_PAIR[0] - 1:
-                for t in range(B_TILES):
-                    p_banks[1, t] = psum_x.tile([P, BANK], F32, name="p_late", tag="x")
-                    for k in PROJECTION_PASSES:
-                        if k not in LAST_PAIR:
-                            multiply(k, 1, t, p_banks[1, t], PROJECTION_PASSES)
-            if n_lo == BANK:
-                for t in range(B_TILES):
-                    multiply(i, 1, t, p_banks[1, t], PROJECTION_PASSES)
+        def add_bias(t):
+            nc.vector.tensor_tensor(out=gate[:, t, :], in0=xz_raw[:, t, :], in1=b_all[:], op=ADD)
 
-            if i == LAST_PAIR[-1]:
-                half = n_lo // BANK
-                n_cols = slice(n_lo, n_hi)
-                for t in range(B_TILES):
-                    nc.vector.tensor_tensor(
-                        out=gate[:, t, n_cols], in0=p_banks[half, t][:], in1=gate[:, t, n_cols], op=MULT
-                    )
-                    nc.sync.dma_start(out=out_view[:, t, n_cols], in_=gate[:, t, n_cols])
+        def leave_gate_bank(k):
+            nc.vector.tensor_tensor(out=gate_view(k), in0=o_banks[k][:], in1=gate_view(k), op=ADD)
+
+        def tanh_gate(k):
+            nc.scalar.activation(out=gate_view(k), in_=gate_view(k), func=TANH)
+
+        def finish(k):
+            half, t = divmod(k, B_TILES)
+            nc.vector.tensor_tensor(out=gate_view(k), in0=p_banks[k][:], in1=gate_view(k), op=MULT)
+            nc.sync.dma_start(out=out_view[:, t, half * BANK : (half + 1) * BANK], in_=gate_view(k))
+
+        grouped_of = {}
+
+        def stage_tile(key, name, width):
+            grouped_of[key] = act_stage.tile([P, width], BF16, name=name, tag="act", align_bytes=64)
+            return grouped_of[key][:]
+
+        tanh_grouped = {}
+
+
+        def c_tile(t):
+            lay_out(c_raw[:, t, :].bitcast(F32), 2, stage_tile(("c", t), "c_grouped", H), nc.vector.tensor_copy, psum_x, "x")
+
+        def tanh_c(t):
+            tanh_grouped[t] = tanh_stage.tile([P, H], BF16, name="tanh_grouped", align_bytes=64)
+            nc.scalar.activation(out=tanh_grouped[t][:], in_=grouped_of["c", t][:], func=TANH)
+
+        def q_c(t):
+            quantise_activation(t, FIRST_C, 2, grouped_of["c", t][:])
+
+        def q_tanh(t):
+            quantise_activation(t, FIRST_TANH_C, 2, tanh_grouped[t][:])
+
+        def h_tile(t):
+            lay_out(h_raw[:, t, :].bitcast(F32), 2, stage_tile(("h", t), "h_grouped", H), nc.vector.tensor_copy, psum_x, "x")
+
+        def q_h(t):
+            quantise_activation(t, FIRST_H, 2, grouped_of["h", t][:])
+
+        def x_tile(t):
+            lay_out(
+                x_raw[t // 2][:, t % 2, :].bitcast(F32), 4, stage_tile(("x", t), "x_grouped", D), nc.scalar.copy, psum_x, "x"
+            )
+
+        def q_x(t):
+            quantise_activation(t, FIRST_X, 4, grouped_of["x", t][:])
+
+        def o_tile(k):
+            o_banks[k] = psum_g.tile([P, BANK], F32, name="o_bank", tag="g")
+            for i in GATE_PASSES:
+                multiply(i, k, o_banks[k], GATE_PASSES)
+
+        def p_pass(i, ks):
+            for k in ks:
+                if i == PROJECTION_PASSES[0]:
+                    if k < X_BANKS:
+                        p_banks[k] = psum_x.tile([P, BANK], F32, name="p_bank", tag="x")
+                    else:
+                        p_banks[k] = psum_g.tile([P, BANK], F32, name="p_late", tag="g")
+                multiply(i, k, p_banks[k], PROJECTION_PASSES)
+
+        for t in range(B_TILES):
+            c_tile(t)
+            tanh_c(t)
+            q_c(t - 1) if t > 0 else None
+        regroup(0, 0, H)
+        q_c(3)
+        q_tanh(0)
+        q_tanh(1)
+        regroup(1, 0, H)
+        h_tile(0)
+        quantise_weights(0, 0, H)
+        q_h(0)
+        h_tile(1)
+        h_tile(2)
+        q_h(1)
+        h_tile(3)
+        q_h(2)
+        spread_bias()
+        quantise_weights(1, 0, H)
+        regroup(2, 0, H)
+        q_tanh(2)
+        q_tanh(3)
+        q_h(3)
+        regroup(3, 0, H)
+        quantise_weights(2, 0, H)
+        add_bias(0)
+        add_bias(1)
+        x_tile(0)
+        quantise_weights(3, 0, H)
+        add_bias(2)
+        x_tile(1)
+        x_tile(2)
+        x_tile(3)
+        q_x(0)
+        for k in range(2):
+            o_tile(k)
+        add_bias(3)
+        q_x(1)
+        leave_gate_bank(0)
+        regroup(4, 0, H)
+        leave_gate_bank(1)
+        for k in range(2, 4):
+            o_tile(k)
+        q_x(2)
+        leave_gate_bank(2)
+        regroup(5, 0, H)
+        quantise_weights(4, 0, H)
+        leave_gate_bank(3)
+        for k in range(4, 6):
+            o_tile(k)
+        q_x(3)
+        leave_gate_bank(4)
+        quantise_weights(5, 0, H)
+        leave_gate_bank(5)
+        regroup(6, 0, H)
+        for k in range(6, 8):
+            o_tile(k)
+        p_pass(4, range(6))
+        leave_gate_bank(6)
+        leave_gate_bank(7)
+        p_pass(5, range(6))
+        regroup(7, 0, H)
+        quantise_weights(6, 0, H)
+        p_pass(4, range(6, 8))
+        p_pass(5, range(6, 8))
+        p_pass(6, range(8))
+        for k in range(2):
+            tanh_gate(k)
+        regroup(8, 0, BANK)
+        quantise_weights(7, 0, H)
+        p_pass(7, range(8))
+        for k in range(2, 4):
+            tanh_gate(k)
+        regroup(9, 0, BANK)
+        quantise_weights(8, 0, BANK)
+        p_pass(8, range(4))
+        regroup(8, BANK, H)
+        quantise_weights(9, 0, BANK)
+        p_pass(9, range(4))
+        regroup(9, BANK, H)
+        quantise_weights(8, BANK, H)
+        for k in range(4, TILES):
+            tanh_gate(k)
+        p_pass(8, range(4, TILES))
+        quantise_weights(9, BANK, H)
+        for k in range(4):
+            finish(k)
+        p_pass(9, range(4, TILES))
+        for k in range(4, TILES):
+            finish(k)

@@ -29,8 +29,8 @@ GATE_PASSES = (0, 1, 2, 3)
 PROJECTION_PASSES = (4, 5, 6, 7, 8, 9)
 LAST_PAIR = (8, 9)
 
-PE_COLS = (512, 512, 512, 512, 512, 512, 0, 0, 0, 0)
-V_COLS = (512, 448, 192, 192, 128, 128, 448, 448, 512, 512)
+PE_COLS = (0, 0, 0, 0, 0, 0, 0, 0, 0, 0)
+V_COLS = (512, 448, 384, 384, 384, 384, 448, 448, 512, 512)
 PE_CHUNK = 256
 
 RAW_BUFS = 11

@@ -19,23 +19,29 @@ K_PASS = P * PACK
 B_TILES = B // P
 BANK = 512
 HALVES = H // BANK
+TILES = HALVES * B_TILES
 
-FIRST_C = 0
-FIRST_H = 2
-FIRST_TANH_C = 4
-FIRST_X = 6
-PASSES = 10
+PASS_OF = (
+    ("c", 0),
+    ("c", 1),
+    ("h", 0),
+    ("h", 1),
+    ("tanh", 0),
+    ("tanh", 1),
+    ("x", 0),
+    ("x", 1),
+    ("x", 2),
+    ("x", 3),
+)
+PASSES = len(PASS_OF)
 GATE_PASSES = (0, 1, 2, 3)
 PROJECTION_PASSES = (4, 5, 6, 7, 8, 9)
-LAST_PAIR = (8, 9)
 
-PE_COLS = (0, 0, 0, 0, 0, 0, 0, 0, 0, 0)
-V_COLS = (512, 448, 384, 384, 384, 384, 448, 448, 512, 512)
-PE_CHUNK = 256
+V_COLS = (512, 448, 320, 320, 320, 320, 448, 448, 448, 448)
 
-RAW_BUFS = 11
-G_BANKS = 2
+RAW_BUFS = 10
 X_BANKS = 6
+G_BANKS = 2
 
 FLOPS = 2 * B * H * (H + H + H + D)
 
@@ -47,8 +53,7 @@ def tile_residuallstmcell_pb_kernel(tc, x, xz_o, h_prev, c, w_i, w_ho, w_co, w_c
         keep = ctx.enter_context(tc.tile_pool(name="keep", bufs=1))
         raw_pool = ctx.enter_context(tc.tile_pool(name="raw_pool", bufs=RAW_BUFS))
         act_stage = ctx.enter_context(tc.tile_pool(name="act_stage", bufs=3))
-        tanh_stage = ctx.enter_context(tc.tile_pool(name="tanh_stage", bufs=4))
-        w_stage = ctx.enter_context(tc.tile_pool(name="w_stage", bufs=4))
+        w_stage = ctx.enter_context(tc.tile_pool(name="w_stage", bufs=3))
         psum_x = ctx.enter_context(tc.psum_pool(name="psum_x", bufs=X_BANKS))
         psum_g = ctx.enter_context(tc.psum_pool(name="psum_g", bufs=G_BANKS))
 
@@ -95,8 +100,6 @@ def tile_residuallstmcell_pb_kernel(tc, x, xz_o, h_prev, c, w_i, w_ho, w_co, w_c
 
         ident = keep.tile([P, P], F32, name="ident")
         make_identity(nc, ident[:])
-        ident_bf = keep.tile([P, P], BF16, name="ident_bf")
-        nc.vector.tensor_copy(out=ident_bf[:], in_=ident[:])
 
         table_in = keep.tile([P, 1], F32, name="table_in")
         table_out = keep.tile([P, 1], F32, name="table_out")
@@ -114,15 +117,18 @@ def tile_residuallstmcell_pb_kernel(tc, x, xz_o, h_prev, c, w_i, w_ho, w_co, w_c
                 nc.tensor.matmul(out=b_bank[:], lhsT=ones[:], rhs=b_row[:, n_cols], start=True, stop=True)
                 nc.scalar.copy(out=b_all[:, n_cols], in_=b_bank[:])
 
-        act_codes = keep.tile([P, B_TILES, PASSES, P], U32, name="act_codes", align_bytes=64)
-        act_scales = keep.tile([P, B_TILES, PASSES, P], U8, name="act_scales", align_bytes=64)
+        act_codes = {}
+        act_scales = {}
+        for source, groups in (("c", 2), ("h", 2), ("tanh", 2), ("x", 4)):
+            act_codes[source] = keep.tile([P, B_TILES, groups, P], U32, name="codes_" + source, align_bytes=64)
+            act_scales[source] = keep.tile([P, B_TILES, groups, P], U8, name="scales_" + source, align_bytes=64)
         w_codes = keep.tile([P, PASSES, H], U32, name="w_codes", align_bytes=64)
         w_scales = keep.tile([P, PASSES, H], U8, name="w_scales", align_bytes=64)
 
-        def lay_out(words, groups, grouped, copy, pool, tag):
+        def lay_out(words, groups, grouped, copy):
             grouped_words = grouped.bitcast(F32)
             for pair in range(groups // 2):
-                bank = pool.tile([P, 4, P], F32, name="t_bank", tag=tag)
+                bank = psum_x.tile([P, 4, P], F32, name="t_bank", tag="x")
                 for j in range(4):
                     first = (4 * pair + j) * P
                     nc.tensor.transpose(bank[:, j, :], words[:, first : first + P], ident[:])
@@ -133,47 +139,23 @@ def tile_residuallstmcell_pb_kernel(tc, x, xz_o, h_prev, c, w_i, w_ho, w_co, w_c
                     in_=bank[:].rearrange("q (g u) r -> q g r u", u=2),
                 )
 
-        def quantise_activation(t, first, count, grouped):
+        def quantise_activation(source, t_lo, t_hi, grouped):
             nc.vector.quantize_mx(
-                out=act_codes[:, t, first : first + count, :].rearrange("q g r -> q (g r)").bitcast(FP8X4),
-                scales=act_scales[:, t, first : first + count, :].rearrange("q g r -> q (g r)"),
-                in_=grouped,
+                out=act_codes[source][:, t_lo:t_hi, :, :].rearrange("q t g r -> q (t g r)").bitcast(FP8X4),
+                scales=act_scales[source][:, t_lo:t_hi, :, :].rearrange("q t g r -> q (t g r)"),
+                in_=grouped.rearrange("q t k -> q (t k)"),
             )
+
+        def stage(name):
+            return act_stage.tile([P, B_TILES * H], BF16, name=name, tag="act", align_bytes=64)
 
         w_grouped = {}
 
         def regroup(i, n_lo, n_hi):
-            regroup_tensor(i, n_lo, n_hi)
-            regroup_copies(i, n_lo, n_hi)
-
-        def regroup_tensor(i, n_lo, n_hi):
-            pe_cols = PE_COLS[i] * (n_hi - n_lo) // H
             if i not in w_grouped:
                 w_grouped[i] = w_stage.tile([P, H, PACK], BF16, name="w_grouped", align_bytes=64)
-            for n0 in range(n_lo, n_lo + pe_cols, PE_CHUNK):
-                bank = psum_x.tile([P, PE_CHUNK, PACK], BF16, name="w_bank", tag="x")
-                for part in range(2):
-                    lo = part * (PE_CHUNK // 2)
-                    cols = slice(n0 + lo, n0 + lo + PE_CHUNK // 2)
-                    nc.tensor.matmul(
-                        out=bank[:, lo : lo + PE_CHUNK // 2, :].rearrange("q n j -> q (n j)"),
-                        lhsT=ident_bf[:],
-                        rhs=w_raw[i][:, :, cols].rearrange("q j n -> q n j"),
-                        start=True,
-                        stop=True,
-                    )
-                nc.scalar.copy(out=w_grouped[i][:, n0 : n0 + PE_CHUNK, :], in_=bank[:])
-
-        def regroup_copies(i, n_lo, n_hi):
-            pe_cols = PE_COLS[i] * (n_hi - n_lo) // H
-            v_cols = V_COLS[i] * (n_hi - n_lo) // H
-            if i not in w_grouped:
-                w_grouped[i] = w_stage.tile([P, H, PACK], BF16, name="w_grouped", align_bytes=64)
-            v_lo = n_lo + pe_cols
-            s_lo = v_lo + v_cols
-            for copy, cols in ((nc.vector.tensor_copy, slice(v_lo, s_lo)), (nc.scalar.copy, slice(s_lo, n_hi))):
-                if cols.start == cols.stop:
-                    continue
+            split = n_lo + V_COLS[i] * (n_hi - n_lo) // H
+            for copy, cols in ((nc.vector.tensor_copy, slice(n_lo, split)), (nc.scalar.copy, slice(split, n_hi))):
                 copy(
                     out=w_grouped[i][:, cols, :].rearrange("q (m i) j -> q m j i", i=4),
                     in_=w_raw[i][:, :, cols].rearrange("q j (m i) -> q m j i", i=4),
@@ -188,11 +170,12 @@ def tile_residuallstmcell_pb_kernel(tc, x, xz_o, h_prev, c, w_i, w_ho, w_co, w_c
 
         def multiply(i, k, bank, passes):
             half, t = divmod(k, B_TILES)
+            source, g = PASS_OF[i]
             n_cols = slice(half * BANK, (half + 1) * BANK)
             nc.tensor.matmul_mx(
                 out=bank[:],
-                lhsT=act_codes[:, t, i, :].bitcast(FP8X4),
-                lhsT_scale=act_scales[:, t, i, :],
+                lhsT=act_codes[source][:, t, g, :].bitcast(FP8X4),
+                lhsT_scale=act_scales[source][:, t, g, :],
                 rhs=w_codes[:, i, n_cols].bitcast(FP8X4),
                 rhs_scale=w_scales[:, i, n_cols],
                 start=(i == passes[0]),
@@ -201,7 +184,6 @@ def tile_residuallstmcell_pb_kernel(tc, x, xz_o, h_prev, c, w_i, w_ho, w_co, w_c
 
         gate = keep.tile([P, B_TILES, H], F32, name="gate")
         out_view = out.rearrange("(p t) n -> p t n", t=B_TILES)
-        TILES = HALVES * B_TILES
         o_banks = {}
         p_banks = {}
 
@@ -209,55 +191,41 @@ def tile_residuallstmcell_pb_kernel(tc, x, xz_o, h_prev, c, w_i, w_ho, w_co, w_c
             half, t = divmod(k, B_TILES)
             return gate[:, t, half * BANK : (half + 1) * BANK]
 
-        def add_bias(t):
-            nc.vector.tensor_tensor(out=gate[:, t, :], in0=xz_raw[:, t, :], in1=b_all[:], op=ADD)
+        def add_bias(t_lo, t_hi):
+            nc.vector.tensor_tensor(
+                out=gate[:, t_lo:t_hi, :],
+                in0=xz_raw[:, t_lo:t_hi, :],
+                in1=b_all[:].unsqueeze(1).to_broadcast([P, t_hi - t_lo, H]),
+                op=ADD,
+            )
 
         def leave_gate_bank(k):
             nc.vector.tensor_tensor(out=gate_view(k), in0=o_banks[k][:], in1=gate_view(k), op=ADD)
 
-        def tanh_gate(k):
-            nc.scalar.activation(out=gate_view(k), in_=gate_view(k), func=TANH)
+        def tanh_gate(half):
+            n_cols = slice(half * BANK, (half + 1) * BANK)
+            nc.scalar.activation(out=gate[:, :, n_cols], in_=gate[:, :, n_cols], func=TANH)
 
         def finish(k):
             half, t = divmod(k, B_TILES)
             nc.vector.tensor_tensor(out=gate_view(k), in0=p_banks[k][:], in1=gate_view(k), op=MULT)
             nc.sync.dma_start(out=out_view[:, t, half * BANK : (half + 1) * BANK], in_=gate_view(k))
 
-        grouped_of = {}
-
-        def stage_tile(key, name, width):
-            grouped_of[key] = act_stage.tile([P, width], BF16, name=name, tag="act", align_bytes=64)
-            return grouped_of[key][:]
-
-        tanh_grouped = {}
-
+        c_grouped = stage("c_grouped")[:].rearrange("q (t k) -> q t k", t=B_TILES)
+        tanh_tile = keep.tile([P, B_TILES * H], BF16, name="tanh_tile", align_bytes=64)
+        tanh_grouped = tanh_tile[:].rearrange("q (t k) -> q t k", t=B_TILES)
 
         def c_tile(t):
-            lay_out(c_raw[:, t, :].bitcast(F32), 2, stage_tile(("c", t), "c_grouped", H), nc.vector.tensor_copy, psum_x, "x")
+            lay_out(c_raw[:, t, :].bitcast(F32), 2, c_grouped[:, t, :], nc.vector.tensor_copy)
 
-        def tanh_c(t):
-            tanh_grouped[t] = tanh_stage.tile([P, H], BF16, name="tanh_grouped", align_bytes=64)
-            nc.scalar.activation(out=tanh_grouped[t][:], in_=grouped_of["c", t][:], func=TANH)
-
-        def q_c(t):
-            quantise_activation(t, FIRST_C, 2, grouped_of["c", t][:])
-
-        def q_tanh(t):
-            quantise_activation(t, FIRST_TANH_C, 2, tanh_grouped[t][:])
+        def tanh_c(t_lo, t_hi):
+            nc.scalar.activation(out=tanh_grouped[:, t_lo:t_hi, :], in_=c_grouped[:, t_lo:t_hi, :], func=TANH)
 
         def h_tile(t):
-            lay_out(h_raw[:, t, :].bitcast(F32), 2, stage_tile(("h", t), "h_grouped", H), nc.vector.tensor_copy, psum_x, "x")
-
-        def q_h(t):
-            quantise_activation(t, FIRST_H, 2, grouped_of["h", t][:])
+            lay_out(h_raw[:, t, :].bitcast(F32), 2, h_grouped[:, t, :], nc.vector.tensor_copy)
 
         def x_tile(t):
-            lay_out(
-                x_raw[t // 2][:, t % 2, :].bitcast(F32), 4, stage_tile(("x", t), "x_grouped", D), nc.scalar.copy, psum_x, "x"
-            )
-
-        def q_x(t):
-            quantise_activation(t, FIRST_X, 4, grouped_of["x", t][:])
+            lay_out(x_raw[t // 2][:, t % 2, :].bitcast(F32), 4, x_grouped[t // 2][:, t % 2, :], nc.scalar.copy)
 
         def o_tile(k):
             o_banks[k] = psum_g.tile([P, BANK], F32, name="o_bank", tag="g")
@@ -273,57 +241,54 @@ def tile_residuallstmcell_pb_kernel(tc, x, xz_o, h_prev, c, w_i, w_ho, w_co, w_c
                         p_banks[k] = psum_g.tile([P, BANK], F32, name="p_late", tag="g")
                 multiply(i, k, p_banks[k], PROJECTION_PASSES)
 
-        for t in range(B_TILES):
-            c_tile(t)
-            tanh_c(t)
-            q_c(t - 1) if t > 0 else None
+        c_tile(0)
+        tanh_c(0, 1)
+        c_tile(1)
+        tanh_c(1, 2)
+        c_tile(2)
+        quantise_activation("c", 0, 2, c_grouped[:, 0:2, :])
+        c_tile(3)
+        tanh_c(2, 4)
         regroup(0, 0, H)
-        q_c(3)
-        q_tanh(0)
-        q_tanh(1)
+        quantise_activation("c", 2, 4, c_grouped[:, 2:4, :])
         regroup(1, 0, H)
+        h_grouped = stage("h_grouped")[:].rearrange("q (t k) -> q t k", t=B_TILES)
         h_tile(0)
-        quantise_weights(0, 0, H)
-        q_h(0)
         h_tile(1)
+        quantise_weights(0, 0, H)
         h_tile(2)
-        q_h(1)
         h_tile(3)
-        q_h(2)
         spread_bias()
-        quantise_weights(1, 0, H)
+        quantise_activation("tanh", 0, 4, tanh_grouped)
+        quantise_activation("h", 0, 4, h_grouped)
         regroup(2, 0, H)
-        q_tanh(2)
-        q_tanh(3)
-        q_h(3)
+        quantise_weights(1, 0, H)
         regroup(3, 0, H)
         quantise_weights(2, 0, H)
-        add_bias(0)
-        add_bias(1)
+        x_grouped = [stage("x_grouped")[:].rearrange("q (t k) -> q t k", t=2)]
+        add_bias(0, 2)
         x_tile(0)
         quantise_weights(3, 0, H)
-        add_bias(2)
         x_tile(1)
+        add_bias(2, 4)
+        x_grouped.append(stage("x_grouped")[:].rearrange("q (t k) -> q t k", t=2))
         x_tile(2)
         x_tile(3)
-        q_x(0)
+        quantise_activation("x", 0, 2, x_grouped[0])
         for k in range(2):
             o_tile(k)
-        add_bias(3)
-        q_x(1)
         leave_gate_bank(0)
         regroup(4, 0, H)
         leave_gate_bank(1)
         for k in range(2, 4):
             o_tile(k)
-        q_x(2)
         leave_gate_bank(2)
         regroup(5, 0, H)
         quantise_weights(4, 0, H)
         leave_gate_bank(3)
         for k in range(4, 6):
             o_tile(k)
-        q_x(3)
+        quantise_activation("x", 2, 4, x_grouped[1])
         leave_gate_bank(4)
         quantise_weights(5, 0, H)
         leave_gate_bank(5)
@@ -339,26 +304,21 @@ def tile_residuallstmcell_pb_kernel(tc, x, xz_o, h_prev, c, w_i, w_ho, w_co, w_c
         p_pass(4, range(6, 8))
         p_pass(5, range(6, 8))
         p_pass(6, range(8))
-        for k in range(2):
-            tanh_gate(k)
-        regroup(8, 0, BANK)
+        regroup(8, 0, H)
         quantise_weights(7, 0, H)
         p_pass(7, range(8))
-        for k in range(2, 4):
-            tanh_gate(k)
+        tanh_gate(0)
         regroup(9, 0, BANK)
-        quantise_weights(8, 0, BANK)
+        quantise_weights(8, 0, H)
         p_pass(8, range(4))
-        regroup(8, BANK, H)
+        regroup(9, BANK, H)
         quantise_weights(9, 0, BANK)
         p_pass(9, range(4))
-        regroup(9, BANK, H)
-        quantise_weights(8, BANK, H)
-        for k in range(4, TILES):
-            tanh_gate(k)
         p_pass(8, range(4, TILES))
+        tanh_gate(1)
+        finish(0)
         quantise_weights(9, BANK, H)
-        for k in range(4):
+        for k in range(1, 4):
             finish(k)
         p_pass(9, range(4, TILES))
         for k in range(4, TILES):

@@ -37,11 +37,13 @@ PASSES = len(PASS_OF)
 GATE_PASSES = (0, 1, 2, 3)
 PROJECTION_PASSES = (4, 5, 6, 7, 8, 9)
 
-V_COLS = (512, 448, 320, 320, 320, 320, 448, 448, 448, 448)
+PE_COLS = (0, 0, 0, 0, 0, 0, 0, 0, 0, 0)
+PE_CHUNK = 256
+V_COLS = (640, 576, 576, 576, 640, 448, 448, 448, 576, 576)
 
 RAW_BUFS = 10
-X_BANKS = 6
-G_BANKS = 2
+X_BANKS = 4
+G_BANKS = 4
 
 FLOPS = 2 * B * H * (H + H + H + D)
 
@@ -92,10 +94,13 @@ def tile_residuallstmcell_pb_kernel(tc, x, xz_o, h_prev, c, w_i, w_ho, w_co, w_c
         nc.sync.dma_start(out=b_row[0:1, :], in_=b_o.rearrange("(o n) -> o n", o=1))
         h_raw = load_rows(h_prev, 0, B_TILES, 2)
         load_weight_pass(2)
-        load_weight_pass(3)
         xz_raw = load_rows(xz_o, 0, B_TILES, 1)
-        x_raw = [load_rows(x, 0, 2, 2), load_rows(x, 2, 2, 2)]
-        for i in range(4, PASSES):
+        load_weight_pass(3)
+        load_weight_pass(4)
+        x_raw = [load_rows(x, 0, 2, 2)]
+        load_weight_pass(5)
+        x_raw.append(load_rows(x, 2, 2, 2))
+        for i in range(6, PASSES):
             load_weight_pass(i)
 
         ident = keep.tile([P, P], F32, name="ident")
@@ -106,16 +111,10 @@ def tile_residuallstmcell_pb_kernel(tc, x, xz_o, h_prev, c, w_i, w_ho, w_co, w_c
         nc.vector.memset(table_in[:], 0.0)
         nc.scalar.activation(out=table_out[:], in_=table_in[:], func=TANH)
 
+        ident_bf = keep.tile([P, P], BF16, name="ident_bf")
+        nc.vector.tensor_copy(out=ident_bf[:], in_=ident[:])
         ones = keep.tile([P, P], BF16, name="ones")
-        b_all = keep.tile([P, H], F32, name="b_all")
         nc.vector.memset(ones[:], 1.0)
-
-        def spread_bias():
-            for half in range(HALVES):
-                n_cols = slice(half * BANK, (half + 1) * BANK)
-                b_bank = psum_x.tile([P, BANK], F32, name="b_bank", tag="x")
-                nc.tensor.matmul(out=b_bank[:], lhsT=ones[:], rhs=b_row[:, n_cols], start=True, stop=True)
-                nc.scalar.copy(out=b_all[:, n_cols], in_=b_bank[:])
 
         act_codes = {}
         act_scales = {}
@@ -154,12 +153,29 @@ def tile_residuallstmcell_pb_kernel(tc, x, xz_o, h_prev, c, w_i, w_ho, w_co, w_c
         def regroup(i, n_lo, n_hi):
             if i not in w_grouped:
                 w_grouped[i] = w_stage.tile([P, H, PACK], BF16, name="w_grouped", align_bytes=64)
-            split = n_lo + V_COLS[i] * (n_hi - n_lo) // H
-            for copy, cols in ((nc.vector.tensor_copy, slice(n_lo, split)), (nc.scalar.copy, slice(split, n_hi))):
+            banks = []
+            for n0 in range(n_lo, n_lo + PE_COLS[i], PE_CHUNK):
+                bank = psum_x.tile([P, PE_CHUNK, PACK], BF16, name="w_bank", tag="x")
+                for u in range(2):
+                    nc.tensor.matmul(
+                        out=bank[:, :, 2 * u : 2 * u + 2].rearrange("q n e -> q e n"),
+                        lhsT=ident_bf[:],
+                        rhs=w_raw[i][:, 2 * u : 2 * u + 2, n0 : n0 + PE_CHUNK],
+                        start=True,
+                        stop=True,
+                    )
+                banks.append((n0, bank))
+            first = n_lo + PE_COLS[i]
+            split = first + V_COLS[i] * (n_hi - n_lo) // H
+            for copy, cols in ((nc.vector.tensor_copy, slice(first, split)), (nc.scalar.copy, slice(split, n_hi))):
+                if cols.start == cols.stop:
+                    continue
                 copy(
                     out=w_grouped[i][:, cols, :].rearrange("q (m i) j -> q m j i", i=4),
                     in_=w_raw[i][:, :, cols].rearrange("q j (m i) -> q m j i", i=4),
                 )
+            for n0, bank in banks:
+                nc.scalar.copy(out=w_grouped[i][:, n0 : n0 + PE_CHUNK, :], in_=bank[:])
 
         def quantise_weights(i, n_lo, n_hi):
             nc.vector.quantize_mx(
@@ -191,13 +207,13 @@ def tile_residuallstmcell_pb_kernel(tc, x, xz_o, h_prev, c, w_i, w_ho, w_co, w_c
             half, t = divmod(k, B_TILES)
             return gate[:, t, half * BANK : (half + 1) * BANK]
 
-        def add_bias(t_lo, t_hi):
-            nc.vector.tensor_tensor(
-                out=gate[:, t_lo:t_hi, :],
-                in0=xz_raw[:, t_lo:t_hi, :],
-                in1=b_all[:].unsqueeze(1).to_broadcast([P, t_hi - t_lo, H]),
-                op=ADD,
-            )
+        def add_bias(t):
+            for k in (t, B_TILES + t):
+                n_cols = slice(k // B_TILES * BANK, (k // B_TILES + 1) * BANK)
+                bank = psum_x.tile([P, BANK], F32, name="xz_bank", tag="x")
+                nc.tensor.matmul(out=bank[:], lhsT=ident_bf[:], rhs=xz_raw[:, t, n_cols], start=True, stop=False)
+                nc.tensor.matmul(out=bank[:], lhsT=ones[:], rhs=b_row[:, n_cols], start=False, stop=True)
+                nc.scalar.copy(out=gate_view(k), in_=bank[:])
 
         def leave_gate_bank(k):
             nc.vector.tensor_tensor(out=gate_view(k), in0=o_banks[k][:], in1=gate_view(k), op=ADD)
@@ -227,6 +243,12 @@ def tile_residuallstmcell_pb_kernel(tc, x, xz_o, h_prev, c, w_i, w_ho, w_co, w_c
         def x_tile(t):
             lay_out(x_raw[t // 2][:, t % 2, :].bitcast(F32), 4, x_grouped[t // 2][:, t % 2, :], nc.scalar.copy)
 
+        def o_pass(i):
+            for k in range(B_TILES):
+                if i == GATE_PASSES[0]:
+                    o_banks[k] = psum_g.tile([P, BANK], F32, name="o_bank", tag="g")
+                multiply(i, k, o_banks[k], GATE_PASSES)
+
         def o_tile(k):
             o_banks[k] = psum_g.tile([P, BANK], F32, name="o_bank", tag="g")
             for i in GATE_PASSES:
@@ -235,7 +257,7 @@ def tile_residuallstmcell_pb_kernel(tc, x, xz_o, h_prev, c, w_i, w_ho, w_co, w_c
         def p_pass(i, ks):
             for k in ks:
                 if i == PROJECTION_PASSES[0]:
-                    if k < X_BANKS:
+                    if k < B_TILES:
                         p_banks[k] = psum_x.tile([P, BANK], F32, name="p_bank", tag="x")
                     else:
                         p_banks[k] = psum_g.tile([P, BANK], F32, name="p_late", tag="g")
@@ -258,51 +280,50 @@ def tile_residuallstmcell_pb_kernel(tc, x, xz_o, h_prev, c, w_i, w_ho, w_co, w_c
         quantise_weights(0, 0, H)
         h_tile(2)
         h_tile(3)
-        spread_bias()
-        quantise_activation("tanh", 0, 4, tanh_grouped)
+        o_pass(0)
         quantise_activation("h", 0, 4, h_grouped)
         regroup(2, 0, H)
+        add_bias(0)
         quantise_weights(1, 0, H)
+        add_bias(1)
+        o_pass(1)
+        quantise_activation("tanh", 0, 4, tanh_grouped)
         regroup(3, 0, H)
+        add_bias(2)
         quantise_weights(2, 0, H)
-        x_grouped = [stage("x_grouped")[:].rearrange("q (t k) -> q t k", t=2)]
-        add_bias(0, 2)
-        x_tile(0)
-        quantise_weights(3, 0, H)
-        x_tile(1)
-        add_bias(2, 4)
-        x_grouped.append(stage("x_grouped")[:].rearrange("q (t k) -> q t k", t=2))
-        x_tile(2)
-        x_tile(3)
-        quantise_activation("x", 0, 2, x_grouped[0])
-        for k in range(2):
-            o_tile(k)
-        leave_gate_bank(0)
+        add_bias(3)
+        o_pass(2)
         regroup(4, 0, H)
-        leave_gate_bank(1)
-        for k in range(2, 4):
-            o_tile(k)
-        leave_gate_bank(2)
-        regroup(5, 0, H)
+        x_grouped = [stage("x_grouped")[:].rearrange("q (t k) -> q t k", t=2)]
+        x_grouped.append(stage("x_grouped")[:].rearrange("q (t k) -> q t k", t=2))
+        quantise_weights(3, 0, H)
+        x_tile(0)
+        o_pass(3)
         quantise_weights(4, 0, H)
-        leave_gate_bank(3)
-        for k in range(4, 6):
-            o_tile(k)
-        quantise_activation("x", 2, 4, x_grouped[1])
-        leave_gate_bank(4)
+        x_tile(1)
+        regroup(5, 0, H)
+        for k in range(4):
+            leave_gate_bank(k)
+        o_tile(4)
+        x_tile(2)
+        quantise_activation("x", 0, 2, x_grouped[0])
+        o_tile(5)
+        x_tile(3)
         quantise_weights(5, 0, H)
+        leave_gate_bank(4)
+        o_tile(6)
+        o_tile(7)
+        p_pass(4, range(4))
         leave_gate_bank(5)
         regroup(6, 0, H)
-        for k in range(6, 8):
-            o_tile(k)
-        p_pass(4, range(6))
+        p_pass(5, range(4))
         leave_gate_bank(6)
         leave_gate_bank(7)
-        p_pass(5, range(6))
+        p_pass(4, range(4, 8))
+        p_pass(5, range(4, 8))
         regroup(7, 0, H)
+        quantise_activation("x", 2, 4, x_grouped[1])
         quantise_weights(6, 0, H)
-        p_pass(4, range(6, 8))
-        p_pass(5, range(6, 8))
         p_pass(6, range(8))
         regroup(8, 0, H)
         quantise_weights(7, 0, H)
@@ -316,9 +337,8 @@ def tile_residuallstmcell_pb_kernel(tc, x, xz_o, h_prev, c, w_i, w_ho, w_co, w_c
         p_pass(9, range(4))
         p_pass(8, range(4, TILES))
         tanh_gate(1)
-        finish(0)
         quantise_weights(9, BANK, H)
-        for k in range(1, 4):
+        for k in range(4):
             finish(k)
         p_pass(9, range(4, TILES))
         for k in range(4, TILES):

@@ -39,7 +39,7 @@ PROJECTION_PASSES = (4, 5, 6, 7, 8, 9)
 
 PE_COLS = (0, 0, 0, 0, 0, 0, 0, 0, 0, 0)
 PE_CHUNK = 256
-V_COLS = (640, 576, 576, 576, 640, 448, 448, 448, 576, 576)
+V_COLS = (640, 576, 576, 576, 640, 448, 384, 384, 512, 512)
 
 RAW_BUFS = 10
 X_BANKS = 4
@@ -219,8 +219,8 @@ def tile_residuallstmcell_pb_kernel(tc, x, xz_o, h_prev, c, w_i, w_ho, w_co, w_c
             nc.vector.tensor_tensor(out=gate_view(k), in0=o_banks[k][:], in1=gate_view(k), op=ADD)
 
         def tanh_gate(half):
-            n_cols = slice(half * BANK, (half + 1) * BANK)
-            nc.scalar.activation(out=gate[:, :, n_cols], in_=gate[:, :, n_cols], func=TANH)
+            for k in range(half * B_TILES, (half + 1) * B_TILES):
+                nc.scalar.activation(out=gate_view(k), in_=gate_view(k), func=TANH)
 
         def finish(k):
             half, t = divmod(k, B_TILES)
@@ -301,9 +301,9 @@ def tile_residuallstmcell_pb_kernel(tc, x, xz_o, h_prev, c, w_i, w_ho, w_co, w_c
         o_pass(3)
         quantise_weights(4, 0, H)
         x_tile(1)
-        regroup(5, 0, H)
         for k in range(4):
             leave_gate_bank(k)
+        regroup(5, 0, H)
         o_tile(4)
         x_tile(2)
         quantise_activation("x", 0, 2, x_grouped[0])
@@ -321,18 +321,18 @@ def tile_residuallstmcell_pb_kernel(tc, x, xz_o, h_prev, c, w_i, w_ho, w_co, w_c
         leave_gate_bank(7)
         p_pass(4, range(4, 8))
         p_pass(5, range(4, 8))
-        regroup(7, 0, H)
         quantise_activation("x", 2, 4, x_grouped[1])
         quantise_weights(6, 0, H)
+        regroup(7, 0, H)
         p_pass(6, range(8))
         regroup(8, 0, H)
         quantise_weights(7, 0, H)
         p_pass(7, range(8))
-        tanh_gate(0)
         regroup(9, 0, BANK)
         quantise_weights(8, 0, H)
         p_pass(8, range(4))
         regroup(9, BANK, H)
+        tanh_gate(0)
         quantise_weights(9, 0, BANK)
         p_pass(9, range(4))
         p_pass(8, range(4, TILES))

@@ -39,7 +39,7 @@ PROJECTION_PASSES = (4, 5, 6, 7, 8, 9)
 
 PE_COLS = (0, 0, 0, 0, 0, 0, 0, 0, 0, 0)
 PE_CHUNK = 256
-V_COLS = (640, 576, 576, 576, 640, 448, 384, 384, 512, 512)
+V_COLS = (576, 576, 576, 512, 704, 384, 384, 384, 384, 384)
 
 RAW_BUFS = 10
 X_BANKS = 4
@@ -238,7 +238,8 @@ def tile_residuallstmcell_pb_kernel(tc, x, xz_o, h_prev, c, w_i, w_ho, w_co, w_c
             nc.scalar.activation(out=tanh_grouped[:, t_lo:t_hi, :], in_=c_grouped[:, t_lo:t_hi, :], func=TANH)
 
         def h_tile(t):
-            lay_out(h_raw[:, t, :].bitcast(F32), 2, h_grouped[:, t, :], nc.vector.tensor_copy)
+            copy = nc.vector.tensor_copy if t < 2 else nc.scalar.copy
+            lay_out(h_raw[:, t, :].bitcast(F32), 2, h_grouped[:, t, :], copy)
 
         def x_tile(t):
             lay_out(x_raw[t // 2][:, t % 2, :].bitcast(F32), 4, x_grouped[t // 2][:, t % 2, :], nc.scalar.copy)
@@ -271,8 +272,8 @@ def tile_residuallstmcell_pb_kernel(tc, x, xz_o, h_prev, c, w_i, w_ho, w_co, w_c
         quantise_activation("c", 0, 2, c_grouped[:, 0:2, :])
         c_tile(3)
         tanh_c(2, 4)
-        regroup(0, 0, H)
         quantise_activation("c", 2, 4, c_grouped[:, 2:4, :])
+        regroup(0, 0, H)
         regroup(1, 0, H)
         h_grouped = stage("h_grouped")[:].rearrange("q (t k) -> q t k", t=B_TILES)
         h_tile(0)
@@ -281,8 +282,8 @@ def tile_residuallstmcell_pb_kernel(tc, x, xz_o, h_prev, c, w_i, w_ho, w_co, w_c
         h_tile(2)
         h_tile(3)
         o_pass(0)
-        quantise_activation("h", 0, 4, h_grouped)
         regroup(2, 0, H)
+        quantise_activation("h", 0, 4, h_grouped)
         add_bias(0)
         quantise_weights(1, 0, H)
         add_bias(1)

@@ -39,7 +39,7 @@ PROJECTION_PASSES = (4, 5, 6, 7, 8, 9)
 
 PE_COLS = (0, 0, 0, 0, 0, 0, 0, 0, 0, 0)
 PE_CHUNK = 256
-V_COLS = (576, 576, 576, 512, 704, 384, 384, 384, 384, 384)
+V_COLS = (576, 576, 512, 576, 768, 384, 384, 384, 448, 448)
 
 RAW_BUFS = 10
 X_BANKS = 4
@@ -326,8 +326,8 @@ def tile_residuallstmcell_pb_kernel(tc, x, xz_o, h_prev, c, w_i, w_ho, w_co, w_c
         quantise_weights(6, 0, H)
         regroup(7, 0, H)
         p_pass(6, range(8))
-        regroup(8, 0, H)
         quantise_weights(7, 0, H)
+        regroup(8, 0, H)
         p_pass(7, range(8))
         regroup(9, 0, BANK)
         quantise_weights(8, 0, H)

from contextlib import ExitStack

import concourse.mybir as mybir
from concourse.masks import make_identity

F32 = mybir.dt.float32
BF16 = mybir.dt.bfloat16
U32 = mybir.dt.uint32
U8 = mybir.dt.uint8
FP8X4 = mybir.dt.float8_e4m3fn_x4
ADD = mybir.AluOpType.add
MULT = mybir.AluOpType.mult
TANH = mybir.ActivationFunctionType.Tanh

B, D, H = 512, 2048, 1024
P = 128
PACK = 4
K_PASS = P * PACK
B_TILES = B // P
BANK = 512
HALVES = H // BANK
TILES = HALVES * B_TILES

PASS_OF = (
    ("c", 0),
    ("c", 1),
    ("h", 0),
    ("h", 1),
    ("tanh", 0),
    ("tanh", 1),
    ("x", 0),
    ("x", 1),
    ("x", 2),
    ("x", 3),
)
PASSES = len(PASS_OF)
GATE_PASSES = (0, 1, 2, 3)
PROJECTION_PASSES = (4, 5, 6, 7, 8, 9)

PE_COLS = (0, 0, 0, 0, 0, 0, 0, 0, 0, 0)
PE_CHUNK = 256
V_COLS = (576, 576, 512, 576, 768, 384, 384, 384, 448, 448)

RAW_BUFS = 10
X_BANKS = 4
G_BANKS = 4

FLOPS = 2 * B * H * (H + H + H + D)


def tile_residuallstmcell_pb_kernel(tc, x, xz_o, h_prev, c, w_i, w_ho, w_co, w_c, b_o, out):
    nc = tc.nc
    with ExitStack() as ctx:
        ctx.enter_context(tc.manual_schedule())
        keep = ctx.enter_context(tc.tile_pool(name="keep", bufs=1))
        raw_pool = ctx.enter_context(tc.tile_pool(name="raw_pool", bufs=RAW_BUFS))
        act_stage = ctx.enter_context(tc.tile_pool(name="act_stage", bufs=3))
        w_stage = ctx.enter_context(tc.tile_pool(name="w_stage", bufs=3))
        psum_x = ctx.enter_context(tc.psum_pool(name="psum_x", bufs=X_BANKS))
        psum_g = ctx.enter_context(tc.psum_pool(name="psum_g", bufs=G_BANKS))

        def load_rows(src, t_first, t_count, pieces):
            k_size = src.shape[1]
            raw = raw_pool.tile([P, t_count, k_size], BF16, name="raw", tag="raw")
            rows = src.rearrange("(p t) k -> p t k", t=B_TILES)
            step = t_count // pieces
            for piece in range(pieces):
                lo = piece * step
                nc.sync.dma_start(
                    out=raw[:, lo : lo + step, :], in_=rows[:, t_first + lo : t_first + lo + step, :]
                )
            return raw

        weight_rows = []
        for w, k_size in ((w_co, H), (w_ho, H), (w_c, H), (w_i, D)):
            for g in range(k_size // K_PASS):
                weight_rows.append(w[g * K_PASS : (g + 1) * K_PASS, :])

        w_raw = {}

        def load_weight_pass(i):
            w_raw[i] = raw_pool.tile([P, PACK, H], BF16, name="raw", tag="raw")
            nc.sync.dma_start(
                out=w_raw[i][:].rearrange("q (u e) n -> q u e n", u=2),
                in_=weight_rows[i].rearrange("(u q e) n -> q u e n", u=2, e=2),
            )

        b_row = keep.tile([P, H], BF16, name="b_row")
        nc.vector.memset(b_row[:], 0.0)

        c_raw = load_rows(c, 0, B_TILES, 4)
        load_weight_pass(0)
        load_weight_pass(1)
        nc.sync.dma_start(out=b_row[0:1, :], in_=b_o.rearrange("(o n) -> o n", o=1))
        h_raw = load_rows(h_prev, 0, B_TILES, 2)
        load_weight_pass(2)
        xz_raw = load_rows(xz_o, 0, B_TILES, 1)
        load_weight_pass(3)
        load_weight_pass(4)
        x_raw = [load_rows(x, 0, 2, 2)]
        load_weight_pass(5)
        x_raw.append(load_rows(x, 2, 2, 2))
        for i in range(6, PASSES):
            load_weight_pass(i)

        ident = keep.tile([P, P], F32, name="ident")
        make_identity(nc, ident[:])

        table_in = keep.tile([P, 1], F32, name="table_in")
        table_out = keep.tile([P, 1], F32, name="table_out")
        nc.vector.memset(table_in[:], 0.0)
        nc.scalar.activation(out=table_out[:], in_=table_in[:], func=TANH)

        ident_bf = keep.tile([P, P], BF16, name="ident_bf")
        nc.vector.tensor_copy(out=ident_bf[:], in_=ident[:])
        ones = keep.tile([P, P], BF16, name="ones")
        nc.vector.memset(ones[:], 1.0)

        act_codes = {}
        act_scales = {}
        for source, groups in (("c", 2), ("h", 2), ("tanh", 2), ("x", 4)):
            act_codes[source] = keep.tile([P, B_TILES, groups, P], U32, name="codes_" + source, align_bytes=64)
            act_scales[source] = keep.tile([P, B_TILES, groups, P], U8, name="scales_" + source, align_bytes=64)
        w_codes = keep.tile([P, PASSES, H], U32, name="w_codes", align_bytes=64)
        w_scales = keep.tile([P, PASSES, H], U8, name="w_scales", align_bytes=64)

        def lay_out(words, groups, grouped, copy):
            grouped_words = grouped.bitcast(F32)
            for pair in range(groups // 2):
                bank = psum_x.tile([P, 4, P], F32, name="t_bank", tag="x")
                for j in range(4):
                    first = (4 * pair + j) * P
                    nc.tensor.transpose(bank[:, j, :], words[:, first : first + P], ident[:])
                copy(
                    out=grouped_words[:, pair * BANK : (pair + 1) * BANK].rearrange(
                        "q (g r u) -> q g r u", g=2, u=2
                    ),
                    in_=bank[:].rearrange("q (g u) r -> q g r u", u=2),
                )

        def quantise_activation(source, t_lo, t_hi, grouped):
            nc.vector.quantize_mx(
                out=act_codes[source][:, t_lo:t_hi, :, :].rearrange("q t g r -> q (t g r)").bitcast(FP8X4),
                scales=act_scales[source][:, t_lo:t_hi, :, :].rearrange("q t g r -> q (t g r)"),
                in_=grouped.rearrange("q t k -> q (t k)"),
            )

        def stage(name):
            return act_stage.tile([P, B_TILES * H], BF16, name=name, tag="act", align_bytes=64)

        w_grouped = {}

        def regroup(i, n_lo, n_hi):
            if i not in w_grouped:
                w_grouped[i] = w_stage.tile([P, H, PACK], BF16, name="w_grouped", align_bytes=64)
            banks = []
            for n0 in range(n_lo, n_lo + PE_COLS[i], PE_CHUNK):
                bank = psum_x.tile([P, PE_CHUNK, PACK], BF16, name="w_bank", tag="x")
                for u in range(2):
                    nc.tensor.matmul(
                        out=bank[:, :, 2 * u : 2 * u + 2].rearrange("q n e -> q e n"),
                        lhsT=ident_bf[:],
                        rhs=w_raw[i][:, 2 * u : 2 * u + 2, n0 : n0 + PE_CHUNK],
                        start=True,
                        stop=True,
                    )
                banks.append((n0, bank))
            first = n_lo + PE_COLS[i]
            split = first + V_COLS[i] * (n_hi - n_lo) // H
            for copy, cols in ((nc.vector.tensor_copy, slice(first, split)), (nc.scalar.copy, slice(split, n_hi))):
                if cols.start == cols.stop:
                    continue
                copy(
                    out=w_grouped[i][:, cols, :].rearrange("q (m i) j -> q m j i", i=4),
                    in_=w_raw[i][:, :, cols].rearrange("q j (m i) -> q m j i", i=4),
                )
            for n0, bank in banks:
                nc.scalar.copy(out=w_grouped[i][:, n0 : n0 + PE_CHUNK, :], in_=bank[:])

        def quantise_weights(i, n_lo, n_hi):
            nc.vector.quantize_mx(
                out=w_codes[:, i, n_lo:n_hi].bitcast(FP8X4),
                scales=w_scales[:, i, n_lo:n_hi],
                in_=w_grouped[i][:, n_lo:n_hi, :].rearrange("q n j -> q (n j)"),
            )

        def multiply(i, k, bank, passes):
            half, t = divmod(k, B_TILES)
            source, g = PASS_OF[i]
            n_cols = slice(half * BANK, (half + 1) * BANK)
            nc.tensor.matmul_mx(
                out=bank[:],
                lhsT=act_codes[source][:, t, g, :].bitcast(FP8X4),
                lhsT_scale=act_scales[source][:, t, g, :],
                rhs=w_codes[:, i, n_cols].bitcast(FP8X4),
                rhs_scale=w_scales[:, i, n_cols],
                start=(i == passes[0]),
                stop=(i == passes[-1]),
            )

        gate = keep.tile([P, B_TILES, H], F32, name="gate")
        out_view = out.rearrange("(p t) n -> p t n", t=B_TILES)
        o_banks = {}
        p_banks = {}

        def gate_view(k):
            half, t = divmod(k, B_TILES)
            return gate[:, t, half * BANK : (half + 1) * BANK]

        def add_bias(t):
            for k in (t, B_TILES + t):
                n_cols = slice(k // B_TILES * BANK, (k // B_TILES + 1) * BANK)
                bank = psum_x.tile([P, BANK], F32, name="xz_bank", tag="x")
                nc.tensor.matmul(out=bank[:], lhsT=ident_bf[:], rhs=xz_raw[:, t, n_cols], start=True, stop=False)
                nc.tensor.matmul(out=bank[:], lhsT=ones[:], rhs=b_row[:, n_cols], start=False, stop=True)
                nc.scalar.copy(out=gate_view(k), in_=bank[:])

        def leave_gate_bank(k):
            nc.vector.tensor_tensor(out=gate_view(k), in0=o_banks[k][:], in1=gate_view(k), op=ADD)

        def tanh_gate(half):
            for k in range(half * B_TILES, (half + 1) * B_TILES):
                nc.scalar.activation(out=gate_view(k), in_=gate_view(k), func=TANH)

        def finish(k):
            half, t = divmod(k, B_TILES)
            nc.vector.tensor_tensor(out=gate_view(k), in0=p_banks[k][:], in1=gate_view(k), op=MULT)
            nc.sync.dma_start(out=out_view[:, t, half * BANK : (half + 1) * BANK], in_=gate_view(k))

        c_grouped = stage("c_grouped")[:].rearrange("q (t k) -> q t k", t=B_TILES)
        tanh_tile = keep.tile([P, B_TILES * H], BF16, name="tanh_tile", align_bytes=64)
        tanh_grouped = tanh_tile[:].rearrange("q (t k) -> q t k", t=B_TILES)

        def c_tile(t):
            lay_out(c_raw[:, t, :].bitcast(F32), 2, c_grouped[:, t, :], nc.vector.tensor_copy)

        def tanh_c(t_lo, t_hi):
            nc.scalar.activation(out=tanh_grouped[:, t_lo:t_hi, :], in_=c_grouped[:, t_lo:t_hi, :], func=TANH)

        def h_tile(t):
            copy = nc.vector.tensor_copy if t < 2 else nc.scalar.copy
            lay_out(h_raw[:, t, :].bitcast(F32), 2, h_grouped[:, t, :], copy)

        def x_tile(t):
            lay_out(x_raw[t // 2][:, t % 2, :].bitcast(F32), 4, x_grouped[t // 2][:, t % 2, :], nc.scalar.copy)

        def o_pass(i):
            for k in range(B_TILES):
                if i == GATE_PASSES[0]:
                    o_banks[k] = psum_g.tile([P, BANK], F32, name="o_bank", tag="g")
                multiply(i, k, o_banks[k], GATE_PASSES)

        def o_tile(k):
            o_banks[k] = psum_g.tile([P, BANK], F32, name="o_bank", tag="g")
            for i in GATE_PASSES:
                multiply(i, k, o_banks[k], GATE_PASSES)

        def p_pass(i, ks):
            for k in ks:
                if i == PROJECTION_PASSES[0]:
                    if k < B_TILES:
                        p_banks[k] = psum_x.tile([P, BANK], F32, name="p_bank", tag="x")
                    else:
                        p_banks[k] = psum_g.tile([P, BANK], F32, name="p_late", tag="g")
                multiply(i, k, p_banks[k], PROJECTION_PASSES)

        c_tile(0)
        tanh_c(0, 1)
        c_tile(1)
        tanh_c(1, 2)
        c_tile(2)
        quantise_activation("c", 0, 2, c_grouped[:, 0:2, :])
        c_tile(3)
        tanh_c(2, 4)
        quantise_activation("c", 2, 4, c_grouped[:, 2:4, :])
        regroup(0, 0, H)
        regroup(1, 0, H)
        h_grouped = stage("h_grouped")[:].rearrange("q (t k) -> q t k", t=B_TILES)
        h_tile(0)
        h_tile(1)
        quantise_weights(0, 0, H)
        h_tile(2)
        h_tile(3)
        o_pass(0)
        regroup(2, 0, H)
        quantise_activation("h", 0, 4, h_grouped)
        add_bias(0)
        quantise_weights(1, 0, H)
        add_bias(1)
        o_pass(1)
        quantise_activation("tanh", 0, 4, tanh_grouped)
        regroup(3, 0, H)
        add_bias(2)
        quantise_weights(2, 0, H)
        add_bias(3)
        o_pass(2)
        regroup(4, 0, H)
        x_grouped = [stage("x_grouped")[:].rearrange("q (t k) -> q t k", t=2)]
        x_grouped.append(stage("x_grouped")[:].rearrange("q (t k) -> q t k", t=2))
        quantise_weights(3, 0, H)
        x_tile(0)
        o_pass(3)
        quantise_weights(4, 0, H)
        x_tile(1)
        for k in range(4):
            leave_gate_bank(k)
        regroup(5, 0, H)
        o_tile(4)
        x_tile(2)
        quantise_activation("x", 0, 2, x_grouped[0])
        o_tile(5)
        x_tile(3)
        quantise_weights(5, 0, H)
        leave_gate_bank(4)
        o_tile(6)
        o_tile(7)
        p_pass(4, range(4))
        leave_gate_bank(5)
        regroup(6, 0, H)
        p_pass(5, range(4))
        leave_gate_bank(6)
        leave_gate_bank(7)
        p_pass(4, range(4, 8))
        p_pass(5, range(4, 8))
        quantise_activation("x", 2, 4, x_grouped[1])
        quantise_weights(6, 0, H)
        regroup(7, 0, H)
        p_pass(6, range(8))
        quantise_weights(7, 0, H)
        regroup(8, 0, H)
        p_pass(7, range(8))
        regroup(9, 0, BANK)
        quantise_weights(8, 0, H)
        p_pass(8, range(4))
        regroup(9, BANK, H)
        tanh_gate(0)
        quantise_weights(9, 0, BANK)
        p_pass(9, range(4))
        p_pass(8, range(4, TILES))
        tanh_gate(1)
        quantise_weights(9, BANK, H)
        for k in range(4):
            finish(k)
        p_pass(9, range(4, TILES))
        for k in range(4, TILES):
            finish(k)
